import numpy as np
import ml_dtypes


def mxq(x, axis, fmt="e4m3"):
    dtype, down = {"e4m3": (ml_dtypes.float8_e4m3fn, 7), "e5m2": (ml_dtypes.float8_e5m2, 14)}[fmt]
    v = np.moveaxis(np.asarray(x, np.float32).astype(ml_dtypes.bfloat16).astype(np.float64), axis, -1)
    blocks = v.reshape(v.shape[:-1] + (-1, 32))
    amax = np.abs(blocks).max(-1, keepdims=True)
    byte = np.maximum(np.where(amax > 0, np.frexp(amax)[1] - 1 + 127, 0) - down, 1)
    scale = np.exp2(byte - 127.0)
    codes = (blocks / scale).astype(np.float32).astype(dtype).astype(np.float64)
    return np.moveaxis((codes * scale).reshape(v.shape), -1, axis)


WIDE = False


def mx_kscale(k):
    if not WIDE:
        return np.ones(k)
    levels = np.array([10, -10, 5, -5, 0])
    a = np.random.permutation(np.resize(levels, k // 512 * 4)).reshape(k // 512, 4)
    idx = np.arange(k)
    return np.exp2(a[idx // 512, idx % 128 // 32])


BF16 = ml_dtypes.bfloat16


def bf(x):
    return np.asarray(x, np.float32).astype(BF16)


def f64(x):
    return np.asarray(x).astype(np.float64)


B, S, D, DFF, R = 4, 128, 1024, 4096, 512


def setup_inputs():
    t, r = mx_kscale(DFF), mx_kscale(R)
    v = np.random.standard_normal((B, S, DFF)) * 1.2
    return {"h_gelu": bf(v / (1.0 + np.exp(-1.702 * v)) * t),
            "c_proj_U": bf(np.random.standard_normal((DFF, R)) * 2.0 / np.sqrt(DFF) / t[:, None]),
            "c_proj_S": bf(np.random.uniform(size=R) * r),
            "c_proj_V": bf(np.random.standard_normal((D, R)) / np.sqrt(R) / r[None, :]),
            "c_proj_bias": bf(np.random.standard_normal(D) * 0.3)}


def reference(h_gelu, c_proj_U, c_proj_S, c_proj_V, c_proj_bias):
    us = f64(c_proj_U) * f64(c_proj_S)[None, :]
    w = mxq(us, 1, "e4m3") @ mxq(f64(c_proj_V), 1, "e4m3").T
    return (mxq(f64(h_gelu), 2, "e4m3") @ mxq(w, 0, "e4m3")) + f64(c_proj_bias)

@@ -1,0 +1,223 @@
+from contextlib import ExitStack
+
+import concourse.mybir as mybir
+from concourse.masks import make_identity
+
+F32 = mybir.dt.float32
+BF16 = mybir.dt.bfloat16
+U32 = mybir.dt.uint32
+U8 = mybir.dt.uint8
+FP8X4 = mybir.dt.float8_e4m3fn_x4
+MULT = mybir.AluOpType.mult
+ADD = mybir.AluOpType.add
+
+P = 128
+TOK, D, DFF, R = 512, 1024, 4096, 512
+G = DFF // 512
+FLOPS = 2 * DFF * D * R + 2 * TOK * DFF * D
+NB = 4
+LAG_B = 2
+
+
+def tile_hybridsuperlayer_pb_kernel(tc, h_gelu, c_proj_U, c_proj_S, c_proj_V, c_proj_bias, out):
+    nc = tc.nc
+    h_flat = h_gelu.flatten_outer_dims()
+    out_flat = out.flatten_outer_dims()
+    with ExitStack() as ctx:
+        keep = ctx.enter_context(tc.tile_pool(name="keep", bufs=1))
+        stage = ctx.enter_context(tc.tile_pool(name="stage", bufs=2))
+        psum = ctx.enter_context(tc.psum_pool(name="psum", bufs=1))
+        ctx.enter_context(tc.manual_schedule())
+
+        ident = keep.tile([P, P], F32, name="ident")
+        make_identity(nc, ident[:])
+
+        s4 = keep.tile([P, 2, 2], BF16, name="s4")
+        with nc.allow_non_contiguous_dma(reason="512 singular values, two pairs to a partition"):
+            nc.sync.dma_start(out=s4[:], in_=c_proj_S.rearrange("(u p e) -> p u e", u=2, p=P, e=2))
+        v_sb = [keep.tile([P, 2048], BF16, name="v_sb%d" % hf) for hf in range(2)]
+        u_sb = [keep.tile([P, 2048], BF16, name="u_sb%d" % g) for g in range(G)]
+        h_sb = [keep.tile([P, 2048], BF16, name="h_sb%d" % g) for g in range(G)]
+        bias_bc = keep.tile([P, D], BF16, name="bias_bc")
+
+        def load_v(hf):
+            nc.sync.dma_start(
+                out=v_sb[hf][:].rearrange("p (t r) -> p t r", t=4),
+                in_=c_proj_V[512 * hf : 512 * (hf + 1), :].rearrange("(t p) r -> p t r", p=P),
+            )
+
+        def load_u(g):
+            nc.sync.dma_start(
+                out=u_sb[g][:].rearrange("p (u x) -> p u x", u=2),
+                in_=c_proj_U[512 * g : 512 * (g + 1), :].rearrange("(u p e) r -> p u (e r)", u=2, p=P, e=2),
+            )
+
+        def load_h(g):
+            nc.sync.dma_start(
+                out=h_sb[g][:].rearrange("p (m k) -> p m k", m=4),
+                in_=h_flat[:, 512 * g : 512 * (g + 1)].rearrange("(m p) k -> p m k", p=P),
+            )
+
+        load_v(0)
+        load_u(0)
+        load_u(1)
+        for g in range(G):
+            load_h(g)
+            if g + 2 < G:
+                load_u(g + 2)
+        load_v(1)
+        nc.sync.dma_start(out=bias_bc[:], in_=c_proj_bias.partition_broadcast(P))
+
+        def codes_and_scales(name):
+            codes = keep.tile([P, 512], U32, name=name + "_c", align_bytes=64)
+            scales = keep.tile([P, 512], U8, name=name + "_s", align_bytes=64)
+            return codes, scales
+
+        us_q = [codes_and_scales("us%d" % g) for g in range(G)]
+        h_q = [codes_and_scales("h%d" % g) for g in range(G)]
+        v_q = [codes_and_scales("v%d" % hf) for hf in range(2)]
+
+        count = [0]
+
+        def next_bank():
+            b = count[0] % NB
+            count[0] = count[0] + 1
+            return psum.tile([P, 512], F32, name="w%d" % b, tag="w%d" % b)
+
+        def quantise(grouped, pair):
+            nc.vector.quantize_mx(out=pair[0][:].bitcast(FP8X4), scales=pair[1][:], in_=grouped[:])
+
+        def transpose_rows(src):
+            words = src[:].bitcast(F32)
+            banks = []
+            for half in range(2):
+                bank = next_bank()
+                for j in range(2):
+                    for u in range(2):
+                        nc.tensor.transpose(
+                            bank[:, 256 * u + 128 * j : 256 * u + 128 * j + 128],
+                            words[:, 256 * (2 * half + j) + 128 * u : 256 * (2 * half + j) + 128 * u + 128],
+                            ident[:],
+                        )
+                banks.append(bank)
+            return banks
+
+        def copy_words(banks, tag):
+            grouped = stage.tile([P, 2048], BF16, name=tag, tag=tag, align_bytes=64)
+            for half in range(2):
+                nc.scalar.copy(
+                    out=grouped[:].bitcast(F32)[:, 512 * half : 512 * (half + 1)].rearrange("p (c u) -> p c u", u=2),
+                    in_=banks[half][:].rearrange("p (u c) -> p c u", u=2),
+                )
+            return grouped
+
+        def scale_words(banks):
+            grouped = stage.tile([P, 2048], BF16, name="usg", tag="usg", align_bytes=64)
+            for half in range(2):
+                nc.vector.tensor_tensor(
+                    out=grouped[:, 1024 * half : 1024 * (half + 1)].rearrange("p (c u e) -> p c u e", u=2, e=2),
+                    in0=banks[half][:].bitcast(BF16).rearrange("p (u c e) -> p c u e", u=2, e=2),
+                    in1=s4[:].unsqueeze(1).to_broadcast([P, 256, 2, 2]),
+                    op=MULT,
+                )
+            return grouped
+
+        w_grouped = {}
+        w_q = {}
+        acc = {}
+
+        def stage1_bank(g, hf, db, on_vector):
+            if db == 0:
+                w_grouped[(g, hf)] = stage.tile([P, 2048], BF16, name="wg", tag="wg", bufs=3, align_bytes=64)
+            bank = next_bank()
+            for t in range(4):
+                nc.tensor.matmul_mx(
+                    out=bank[:, 128 * t : 128 * (t + 1)],
+                    lhsT=us_q[g][0][:, 128 * t : 128 * (t + 1)].bitcast(FP8X4),
+                    lhsT_scale=us_q[g][1][:, 128 * t : 128 * (t + 1)],
+                    rhs=v_q[hf][0][:, 128 * db : 128 * (db + 1)].bitcast(FP8X4),
+                    rhs_scale=v_q[hf][1][:, 128 * db : 128 * (db + 1)],
+                    start=True,
+                    stop=True,
+                )
+            dst = w_grouped[(g, hf)][:, 512 * db : 512 * (db + 1)].rearrange("p (d t) -> p d t", t=4)
+            src = bank[:].rearrange("p (t d) -> p d t", t=4)
+            if on_vector:
+                nc.vector.tensor_copy(out=dst, in_=src)
+            else:
+                nc.scalar.copy(out=dst, in_=src)
+
+        def quantise_w(g, hf):
+            codes = keep.tile([P, 512], U32, name="w%d_c" % g, tag="w%d_c" % g, align_bytes=64)
+            scales = keep.tile([P, 512], U8, name="w%d_s" % g, tag="w%d_s" % g, align_bytes=64)
+            w_q[(g, hf)] = (codes, scales)
+            quantise(w_grouped[(g, hf)], w_q[(g, hf)])
+
+        def stage2_pass(g, hf, m):
+            if g == 0:
+                acc[(hf, m)] = psum.tile([P, 512], F32, name="acc%d" % m, tag="acc%d" % m)
+            nc.tensor.matmul_mx(
+                out=acc[(hf, m)][:],
+                lhsT=h_q[g][0][:, 128 * m : 128 * (m + 1)].bitcast(FP8X4),
+                lhsT_scale=h_q[g][1][:, 128 * m : 128 * (m + 1)],
+                rhs=w_q[(g, hf)][0][:].bitcast(FP8X4),
+                rhs_scale=w_q[(g, hf)][1][:],
+                start=(g == 0),
+                stop=(g == G - 1),
+            )
+
+        def finish(hf, m):
+            res = stage.tile([P, 512], F32, name="res", tag="res", bufs=4)
+            nc.vector.tensor_tensor(
+                out=res[:], in0=acc[(hf, m)][:], in1=bias_bc[:, 512 * hf : 512 * (hf + 1)], op=ADD
+            )
+            nc.sync.dma_start(out=out_flat[128 * m : 128 * (m + 1), 512 * hf : 512 * (hf + 1)], in_=res[:])
+
+        vb = transpose_rows(v_sb[0])
+        vg = copy_words(vb, "vg")
+        ub0 = transpose_rows(u_sb[0])
+        ug0 = scale_words(ub0)
+        ub1 = transpose_rows(u_sb[1])
+        quantise(vg, v_q[0])
+        quantise(ug0, us_q[0])
+        ug1 = scale_words(ub1)
+        hb0 = transpose_rows(h_sb[0])
+        hg0 = copy_words(hb0, "hg")
+        hb1 = transpose_rows(h_sb[1])
+        hg1 = copy_words(hb1, "hg")
+        quantise(hg0, h_q[0])
+        quantise(ug1, us_q[1])
+        quantise(hg1, h_q[1])
+
+        for i in range(G):
+            for b in range(4):
+                stage1_bank(i, 0, b, False)
+                if i >= 1:
+                    stage2_pass(i - 1, 0, b)
+            quantise_w(i, 0)
+            if i + 2 < G:
+                hb = transpose_rows(h_sb[i + 2])
+                hg = copy_words(hb, "hg")
+                ub = transpose_rows(u_sb[i + 2])
+                ug = scale_words(ub)
+                quantise(hg, h_q[i + 2])
+                quantise(ug, us_q[i + 2])
+            elif i + 2 == G:
+                vb = transpose_rows(v_sb[1])
+                vg = copy_words(vb, "vg")
+                quantise(vg, v_q[1])
+
+        for j in range(G):
+            for b in range(4):
+                stage1_bank(j, 1, b, b == 0 and j != 1)
+                if j == 0:
+                    stage2_pass(G - 1, 0, b)
+                    finish(0, b)
+                elif j >= LAG_B:
+                    stage2_pass(j - LAG_B, 1, b)
+            quantise_w(j, 1)
+        for g in range(G - LAG_B, G):
+            for m in range(4):
+                stage2_pass(g, 1, m)
+                if g == G - 1:
+                    finish(1, m)

@@ -16,7 +16,10 @@ TOK, D, DFF, R = 512, 1024, 4096, 512
 G = DFF // 512
 FLOPS = 2 * DFF * D * R + 2 * TOK * DFF * D
 NB = 4
-LAG_B = 2
+LAG_A = 2
+EARLY_END = 2
+LAG_B = 3
+VIA_SCALAR = ()
 
 
 def tile_hybridsuperlayer_pb_kernel(tc, h_gelu, c_proj_U, c_proj_S, c_proj_V, c_proj_bias, out):
@@ -58,8 +61,8 @@ def tile_hybridsuperlayer_pb_kernel(tc, h_gelu, c_proj_U, c_proj_S, c_proj_V, c_
                 in_=h_flat[:, 512 * g : 512 * (g + 1)].rearrange("(m p) k -> p m k", p=P),
             )
 
-        load_v(0)
         load_u(0)
+        load_v(0)
         load_u(1)
         for g in range(G):
             load_h(g)
@@ -79,7 +82,15 @@ def tile_hybridsuperlayer_pb_kernel(tc, h_gelu, c_proj_U, c_proj_S, c_proj_V, c_
 
         count = [0]
 
+        early = [True]
+
         def next_bank():
+            if early[0]:
+                b = count[0] % 8
+                count[0] = count[0] + 1
+                if b >= 4:
+                    return psum.tile([P, 512], F32, name="spare%d" % (b - 4), tag="acc%d" % (b - 4))
+                return psum.tile([P, 512], F32, name="w%d" % b, tag="w%d" % b)
             b = count[0] % NB
             count[0] = count[0] + 1
             return psum.tile([P, 512], F32, name="w%d" % b, tag="w%d" % b)
@@ -87,39 +98,46 @@ def tile_hybridsuperlayer_pb_kernel(tc, h_gelu, c_proj_U, c_proj_S, c_proj_V, c_
         def quantise(grouped, pair):
             nc.vector.quantize_mx(out=pair[0][:].bitcast(FP8X4), scales=pair[1][:], in_=grouped[:])
 
-        def transpose_rows(src):
+        def transpose_rows(src, banks):
             words = src[:].bitcast(F32)
-            banks = []
             for half in range(2):
-                bank = next_bank()
                 for j in range(2):
                     for u in range(2):
                         nc.tensor.transpose(
-                            bank[:, 256 * u + 128 * j : 256 * u + 128 * j + 128],
+                            banks[half][:, 256 * u + 128 * j : 256 * u + 128 * j + 128],
                             words[:, 256 * (2 * half + j) + 128 * u : 256 * (2 * half + j) + 128 * u + 128],
                             ident[:],
                         )
-                banks.append(bank)
             return banks
+
+        def copy_bank_words(bank, dst_bf16):
+            nc.scalar.copy(
+                out=dst_bf16.bitcast(F32).rearrange("p (c u) -> p c u", u=2),
+                in_=bank[:].rearrange("p (u c) -> p c u", u=2),
+            )
 
         def copy_words(banks, tag):
             grouped = stage.tile([P, 2048], BF16, name=tag, tag=tag, align_bytes=64)
             for half in range(2):
-                nc.scalar.copy(
-                    out=grouped[:].bitcast(F32)[:, 512 * half : 512 * (half + 1)].rearrange("p (c u) -> p c u", u=2),
-                    in_=banks[half][:].rearrange("p (u c) -> p c u", u=2),
-                )
+                copy_bank_words(banks[half], grouped[:, 1024 * half : 1024 * (half + 1)])
             return grouped
 
-        def scale_words(banks):
+        s4_all = s4[:].unsqueeze(1).to_broadcast([P, 256, 2, 2])
+
+        def scale_words(g, banks):
             grouped = stage.tile([P, 2048], BF16, name="usg", tag="usg", align_bytes=64)
+            raw = {}
             for half in range(2):
-                nc.vector.tensor_tensor(
-                    out=grouped[:, 1024 * half : 1024 * (half + 1)].rearrange("p (c u e) -> p c u e", u=2, e=2),
-                    in0=banks[half][:].bitcast(BF16).rearrange("p (u c e) -> p c u e", u=2, e=2),
-                    in1=s4[:].unsqueeze(1).to_broadcast([P, 256, 2, 2]),
-                    op=MULT,
-                )
+                if (g, half) in VIA_SCALAR:
+                    raw[half] = stage.tile([P, 1024], BF16, name="uraw", tag="uraw", align_bytes=64)
+                    copy_bank_words(banks[half], raw[half][:])
+            for half in range(2):
+                dst = grouped[:, 1024 * half : 1024 * (half + 1)].rearrange("p (c u e) -> p c u e", u=2, e=2)
+                if half in raw:
+                    src = raw[half][:].rearrange("p (c u e) -> p c u e", u=2, e=2)
+                else:
+                    src = banks[half][:].bitcast(BF16).rearrange("p (u c e) -> p c u e", u=2, e=2)
+                nc.vector.tensor_tensor(out=dst, in0=src, in1=s4_all, op=MULT)
             return grouped
 
         w_grouped = {}
@@ -153,6 +171,13 @@ def tile_hybridsuperlayer_pb_kernel(tc, h_gelu, c_proj_U, c_proj_S, c_proj_V, c_
             w_q[(g, hf)] = (codes, scales)
             quantise(w_grouped[(g, hf)], w_q[(g, hf)])
 
+        def finish(hf, m):
+            res = stage.tile([P, 512], F32, name="res", tag="res", bufs=4)
+            nc.vector.tensor_tensor(
+                out=res[:], in0=acc[(hf, m)][:], in1=bias_bc[:, 512 * hf : 512 * (hf + 1)], op=ADD
+            )
+            nc.sync.dma_start(out=out_flat[128 * m : 128 * (m + 1), 512 * hf : 512 * (hf + 1)], in_=res[:])
+
         def stage2_pass(g, hf, m):
             if g == 0:
                 acc[(hf, m)] = psum.tile([P, 512], F32, name="acc%d" % m, tag="acc%d" % m)
@@ -165,59 +190,53 @@ def tile_hybridsuperlayer_pb_kernel(tc, h_gelu, c_proj_U, c_proj_S, c_proj_V, c_
                 start=(g == 0),
                 stop=(g == G - 1),
             )
+            if g == G - 1:
+                finish(hf, m)
 
-        def finish(hf, m):
-            res = stage.tile([P, 512], F32, name="res", tag="res", bufs=4)
-            nc.vector.tensor_tensor(
-                out=res[:], in0=acc[(hf, m)][:], in1=bias_bc[:, 512 * hf : 512 * (hf + 1)], op=ADD
-            )
-            nc.sync.dma_start(out=out_flat[128 * m : 128 * (m + 1), 512 * hf : 512 * (hf + 1)], in_=res[:])
-
-        vb = transpose_rows(v_sb[0])
+        ub0 = transpose_rows(u_sb[0], [next_bank(), next_bank()])
+        ug0 = scale_words(0, ub0)
+        vb = transpose_rows(v_sb[0], [next_bank(), next_bank()])
         vg = copy_words(vb, "vg")
-        ub0 = transpose_rows(u_sb[0])
-        ug0 = scale_words(ub0)
-        ub1 = transpose_rows(u_sb[1])
-        quantise(vg, v_q[0])
+        ub1 = transpose_rows(u_sb[1], [next_bank(), next_bank()])
         quantise(ug0, us_q[0])
-        ug1 = scale_words(ub1)
-        hb0 = transpose_rows(h_sb[0])
-        hg0 = copy_words(hb0, "hg")
-        hb1 = transpose_rows(h_sb[1])
-        hg1 = copy_words(hb1, "hg")
-        quantise(hg0, h_q[0])
+        quantise(vg, v_q[0])
+        ug1 = scale_words(1, ub1)
         quantise(ug1, us_q[1])
-        quantise(hg1, h_q[1])
 
         for i in range(G):
+            if i == EARLY_END:
+                early[0] = False
             for b in range(4):
-                stage1_bank(i, 0, b, False)
-                if i >= 1:
-                    stage2_pass(i - 1, 0, b)
+                stage1_bank(i, 0, b, i == 0 and b % 2 == 1)
+                if i >= LAG_A:
+                    stage2_pass(i - LAG_A, 0, b)
             quantise_w(i, 0)
+            hb = transpose_rows(h_sb[i], [next_bank(), next_bank()])
+            hg = copy_words(hb, "hg")
             if i + 2 < G:
-                hb = transpose_rows(h_sb[i + 2])
-                hg = copy_words(hb, "hg")
-                ub = transpose_rows(u_sb[i + 2])
-                ug = scale_words(ub)
-                quantise(hg, h_q[i + 2])
+                ub = transpose_rows(u_sb[i + 2], [next_bank(), next_bank()])
+                ug = scale_words(i + 2, ub)
+            elif i + 2 == G:
+                vb = transpose_rows(v_sb[1], [next_bank(), next_bank()])
+                vg = copy_words(vb, "vg")
+            quantise(hg, h_q[i])
+            if i + 2 < G:
                 quantise(ug, us_q[i + 2])
             elif i + 2 == G:
-                vb = transpose_rows(v_sb[1])
-                vg = copy_words(vb, "vg")
                 quantise(vg, v_q[1])
 
+        waiting = [(g, 0, m) for g in range(G - LAG_A, G) for m in range(4)]
+        taken = [0]
         for j in range(G):
+            if j >= LAG_B:
+                waiting.extend([(j - LAG_B, 1, m) for m in range(4)])
             for b in range(4):
-                stage1_bank(j, 1, b, b == 0 and j != 1)
-                if j == 0:
-                    stage2_pass(G - 1, 0, b)
-                    finish(0, b)
-                elif j >= LAG_B:
-                    stage2_pass(j - LAG_B, 1, b)
+                stage1_bank(j, 1, b, b == 0 and j != 2)
+                if taken[0] < len(waiting):
+                    stage2_pass(*waiting[taken[0]])
+                    taken[0] = taken[0] + 1
             quantise_w(j, 1)
-        for g in range(G - LAG_B, G):
-            for m in range(4):
-                stage2_pass(g, 1, m)
-                if g == G - 1:
-                    finish(1, m)
+        waiting.extend([(g, 1, m) for g in range(G - LAG_B, G - 2) for m in range(4)])
+        waiting.extend([(g, 1, m) for m in range(4) for g in range(G - 2, G)])
+        for item in waiting[taken[0] :]:
+            stage2_pass(*item)

@@ -19,7 +19,7 @@ NB = 4
 LAG_A = 2
 EARLY_END = 2
 LAG_B = 3
-VIA_SCALAR = ()
+VIA_SCALAR = tuple([(g, 1) for g in range(8)])
 
 
 def tile_hybridsuperlayer_pb_kernel(tc, h_gelu, c_proj_U, c_proj_S, c_proj_V, c_proj_bias, out):

@@ -15,11 +15,12 @@ P = 128
 TOK, D, DFF, R = 512, 1024, 4096, 512
 G = DFF // 512
 FLOPS = 2 * DFF * D * R + 2 * TOK * DFF * D
+VEC_A = {0: (1, 3)}
+VEC_B = {2: ()}
+LAST_PIECES = 1
 NB = 4
 LAG_A = 2
-EARLY_END = 2
 LAG_B = 3
-VIA_SCALAR = tuple([(g, 1) for g in range(8)])
 
 
 def tile_hybridsuperlayer_pb_kernel(tc, h_gelu, c_proj_U, c_proj_S, c_proj_V, c_proj_bias, out):
@@ -38,20 +39,28 @@ def tile_hybridsuperlayer_pb_kernel(tc, h_gelu, c_proj_U, c_proj_S, c_proj_V, c_
         s4 = keep.tile([P, 2, 2], BF16, name="s4")
         with nc.allow_non_contiguous_dma(reason="512 singular values, two pairs to a partition"):
             nc.sync.dma_start(out=s4[:], in_=c_proj_S.rearrange("(u p e) -> p u e", u=2, p=P, e=2))
-        v_sb = [keep.tile([P, 2048], BF16, name="v_sb%d" % hf) for hf in range(2)]
-        u_sb = [keep.tile([P, 2048], BF16, name="u_sb%d" % g) for g in range(G)]
+        v_sb = [keep.tile([P, 1024], BF16, name="v_sb%d" % q) for q in range(4)]
+        u_sb = [keep.tile([P, 1024], BF16, name="u_sb%d" % q) for q in range(2)] + [
+            keep.tile([P, 2048], BF16, name="u_sb%d" % (g + 1)) for g in range(1, G)
+        ]
         h_sb = [keep.tile([P, 2048], BF16, name="h_sb%d" % g) for g in range(G)]
         bias_bc = keep.tile([P, D], BF16, name="bias_bc")
 
-        def load_v(hf):
+        def load_v(q):
             nc.sync.dma_start(
-                out=v_sb[hf][:].rearrange("p (t r) -> p t r", t=4),
-                in_=c_proj_V[512 * hf : 512 * (hf + 1), :].rearrange("(t p) r -> p t r", p=P),
+                out=v_sb[q][:].rearrange("p (t r) -> p t r", t=2),
+                in_=c_proj_V[256 * q : 256 * (q + 1), :].rearrange("(t p) r -> p t r", p=P),
+            )
+
+        def load_u_half(q):
+            nc.sync.dma_start(
+                out=u_sb[q][:],
+                in_=c_proj_U[256 * q : 256 * (q + 1), :].rearrange("(p e) r -> p (e r)", p=P, e=2),
             )
 
         def load_u(g):
             nc.sync.dma_start(
-                out=u_sb[g][:].rearrange("p (u x) -> p u x", u=2),
+                out=u_sb[g + 1][:].rearrange("p (u x) -> p u x", u=2),
                 in_=c_proj_U[512 * g : 512 * (g + 1), :].rearrange("(u p e) r -> p u (e r)", u=2, p=P, e=2),
             )
 
@@ -61,15 +70,26 @@ def tile_hybridsuperlayer_pb_kernel(tc, h_gelu, c_proj_U, c_proj_S, c_proj_V, c_
                 in_=h_flat[:, 512 * g : 512 * (g + 1)].rearrange("(m p) k -> p m k", p=P),
             )
 
-        load_u(0)
+        load_u_half(0)
         load_v(0)
+        load_u_half(1)
+        load_v(1)
         load_u(1)
         for g in range(G):
             load_h(g)
             if g + 2 < G:
                 load_u(g + 2)
-        load_v(1)
+        load_v(2)
+        load_v(3)
         nc.sync.dma_start(out=bias_bc[:], in_=c_proj_bias.partition_broadcast(P))
+
+        def halves(tile_ap):
+            return [tile_ap[:, 0:1024], tile_ap[:, 1024:2048]]
+
+        def u_halves(g):
+            if g == 0:
+                return [u_sb[0][:], u_sb[1][:]]
+            return halves(u_sb[g + 1])
 
         def codes_and_scales(name):
             codes = keep.tile([P, 512], U32, name=name + "_c", align_bytes=64)
@@ -81,63 +101,65 @@ def tile_hybridsuperlayer_pb_kernel(tc, h_gelu, c_proj_U, c_proj_S, c_proj_V, c_
         v_q = [codes_and_scales("v%d" % hf) for hf in range(2)]
 
         count = [0]
-
-        early = [True]
+        banks_in_use = [8]
 
         def next_bank():
-            if early[0]:
-                b = count[0] % 8
-                count[0] = count[0] + 1
-                if b >= 4:
-                    return psum.tile([P, 512], F32, name="spare%d" % (b - 4), tag="acc%d" % (b - 4))
-                return psum.tile([P, 512], F32, name="w%d" % b, tag="w%d" % b)
-            b = count[0] % NB
+            b = count[0] % banks_in_use[0]
             count[0] = count[0] + 1
+            if b >= NB:
+                return psum.tile([P, 512], F32, name="spare%d" % (b - NB), tag="acc%d" % (b - NB))
             return psum.tile([P, 512], F32, name="w%d" % b, tag="w%d" % b)
 
-        def quantise(grouped, pair):
-            nc.vector.quantize_mx(out=pair[0][:].bitcast(FP8X4), scales=pair[1][:], in_=grouped[:])
-
-        def transpose_rows(src, banks):
-            words = src[:].bitcast(F32)
-            for half in range(2):
-                for j in range(2):
-                    for u in range(2):
-                        nc.tensor.transpose(
-                            banks[half][:, 256 * u + 128 * j : 256 * u + 128 * j + 128],
-                            words[:, 256 * (2 * half + j) + 128 * u : 256 * (2 * half + j) + 128 * u + 128],
-                            ident[:],
-                        )
-            return banks
-
-        def copy_bank_words(bank, dst_bf16):
-            nc.scalar.copy(
-                out=dst_bf16.bitcast(F32).rearrange("p (c u) -> p c u", u=2),
-                in_=bank[:].rearrange("p (u c) -> p c u", u=2),
+        def quantise(grouped, pair, lo=0, hi=512):
+            nc.vector.quantize_mx(
+                out=pair[0][:, lo:hi].bitcast(FP8X4), scales=pair[1][:, lo:hi], in_=grouped[:, 4 * lo : 4 * hi]
             )
 
-        def copy_words(banks, tag):
-            grouped = stage.tile([P, 2048], BF16, name=tag, tag=tag, align_bytes=64)
-            for half in range(2):
-                copy_bank_words(banks[half], grouped[:, 1024 * half : 1024 * (half + 1)])
-            return grouped
+        def transpose_half(src):
+            words = src.bitcast(F32)
+            bank = next_bank()
+            for j in range(2):
+                for u in range(2):
+                    nc.tensor.transpose(
+                        bank[:, 256 * u + 128 * j : 256 * u + 128 * j + 128],
+                        words[:, 256 * j + 128 * u : 256 * j + 128 * u + 128],
+                        ident[:],
+                    )
+            return bank
+
+        def copy_bank_words(bank, dst_bf16, on_vector):
+            dst = dst_bf16.bitcast(F32).rearrange("p (c u) -> p c u", u=2)
+            src = bank[:].rearrange("p (u c) -> p c u", u=2)
+            if on_vector:
+                nc.vector.tensor_copy(out=dst, in_=src)
+            else:
+                nc.scalar.copy(out=dst, in_=src)
 
         s4_all = s4[:].unsqueeze(1).to_broadcast([P, 256, 2, 2])
 
-        def scale_words(g, banks):
-            grouped = stage.tile([P, 2048], BF16, name="usg", tag="usg", align_bytes=64)
-            raw = {}
+        def scale_bank(bank, dst_bf16):
+            nc.vector.tensor_tensor(
+                out=dst_bf16.rearrange("p (c u e) -> p c u e", u=2, e=2),
+                in0=bank[:].bitcast(BF16).rearrange("p (u c e) -> p c u e", u=2, e=2),
+                in1=s4_all,
+                op=MULT,
+            )
+
+        def grouped_tile(tag):
+            return stage.tile([P, 2048], BF16, name=tag, tag=tag, align_bytes=64)
+
+        def prepare_u(g):
+            grouped = grouped_tile("usg")
+            banks = [transpose_half(src) for src in u_halves(g)]
             for half in range(2):
-                if (g, half) in VIA_SCALAR:
-                    raw[half] = stage.tile([P, 1024], BF16, name="uraw", tag="uraw", align_bytes=64)
-                    copy_bank_words(banks[half], raw[half][:])
+                scale_bank(banks[half], grouped[:, 1024 * half : 1024 * (half + 1)])
+            return grouped
+
+        def prepare_words(sources, tag, on_vector):
+            grouped = grouped_tile(tag)
+            banks = [transpose_half(src) for src in sources]
             for half in range(2):
-                dst = grouped[:, 1024 * half : 1024 * (half + 1)].rearrange("p (c u e) -> p c u e", u=2, e=2)
-                if half in raw:
-                    src = raw[half][:].rearrange("p (c u e) -> p c u e", u=2, e=2)
-                else:
-                    src = banks[half][:].bitcast(BF16).rearrange("p (u c e) -> p c u e", u=2, e=2)
-                nc.vector.tensor_tensor(out=dst, in0=src, in1=s4_all, op=MULT)
+                copy_bank_words(banks[half], grouped[:, 1024 * half : 1024 * (half + 1)], on_vector[half])
             return grouped
 
         w_grouped = {}
@@ -171,12 +193,21 @@ def tile_hybridsuperlayer_pb_kernel(tc, h_gelu, c_proj_U, c_proj_S, c_proj_V, c_
             w_q[(g, hf)] = (codes, scales)
             quantise(w_grouped[(g, hf)], w_q[(g, hf)])
 
-        def finish(hf, m):
+        def finish(hf, m, pieces):
             res = stage.tile([P, 512], F32, name="res", tag="res", bufs=4)
-            nc.vector.tensor_tensor(
-                out=res[:], in0=acc[(hf, m)][:], in1=bias_bc[:, 512 * hf : 512 * (hf + 1)], op=ADD
-            )
-            nc.sync.dma_start(out=out_flat[128 * m : 128 * (m + 1), 512 * hf : 512 * (hf + 1)], in_=res[:])
+            width = 512 // pieces
+            for c in range(pieces):
+                cols = slice(width * c, width * (c + 1))
+                nc.vector.tensor_tensor(
+                    out=res[:, cols],
+                    in0=acc[(hf, m)][:, cols],
+                    in1=bias_bc[:, 512 * hf + width * c : 512 * hf + width * (c + 1)],
+                    op=ADD,
+                )
+                nc.sync.dma_start(
+                    out=out_flat[128 * m : 128 * (m + 1), 512 * hf + width * c : 512 * hf + width * (c + 1)],
+                    in_=res[:, cols],
+                )
 
         def stage2_pass(g, hf, m):
             if g == 0:
@@ -191,34 +222,38 @@ def tile_hybridsuperlayer_pb_kernel(tc, h_gelu, c_proj_U, c_proj_S, c_proj_V, c_
                 stop=(g == G - 1),
             )
             if g == G - 1:
-                finish(hf, m)
+                finish(hf, m, LAST_PIECES if (hf == 1 and m == 3) else 1)
 
-        ub0 = transpose_rows(u_sb[0], [next_bank(), next_bank()])
-        ug0 = scale_words(0, ub0)
-        vb = transpose_rows(v_sb[0], [next_bank(), next_bank()])
-        vg = copy_words(vb, "vg")
-        ub1 = transpose_rows(u_sb[1], [next_bank(), next_bank()])
+        ug0 = grouped_tile("usg")
+        vg = grouped_tile("vg")
+        bank_u = transpose_half(u_sb[0][:])
+        scale_bank(bank_u, ug0[:, 0:1024])
+        bank_v = transpose_half(v_sb[0][:])
+        copy_bank_words(bank_v, vg[:, 0:1024], False)
+        bank_u = transpose_half(u_sb[1][:])
+        scale_bank(bank_u, ug0[:, 1024:2048])
+        bank_v = transpose_half(v_sb[1][:])
+        copy_bank_words(bank_v, vg[:, 1024:2048], False)
+        quantise(vg, v_q[0], 0, 256)
         quantise(ug0, us_q[0])
-        quantise(vg, v_q[0])
-        ug1 = scale_words(1, ub1)
+        quantise(vg, v_q[0], 256, 512)
+        ug1 = prepare_u(1)
         quantise(ug1, us_q[1])
 
         for i in range(G):
-            if i == EARLY_END:
-                early[0] = False
+            if i == LAG_A:
+                banks_in_use[0] = NB
+                count[0] = 0
             for b in range(4):
-                stage1_bank(i, 0, b, i == 0 and b % 2 == 1)
+                stage1_bank(i, 0, b, b in VEC_A.get(i, ()))
                 if i >= LAG_A:
-                    stage2_pass(i - LAG_A, 0, b)
+                    stage2_pass(i - LAG_A, 0, (b + 2) % 4)
             quantise_w(i, 0)
-            hb = transpose_rows(h_sb[i], [next_bank(), next_bank()])
-            hg = copy_words(hb, "hg")
+            hg = prepare_words(halves(h_sb[i]), "hg", (False, False))
             if i + 2 < G:
-                ub = transpose_rows(u_sb[i + 2], [next_bank(), next_bank()])
-                ug = scale_words(i + 2, ub)
+                ug = prepare_u(i + 2)
             elif i + 2 == G:
-                vb = transpose_rows(v_sb[1], [next_bank(), next_bank()])
-                vg = copy_words(vb, "vg")
+                vg = prepare_words([v_sb[2][:], v_sb[3][:]], "vg", (True, True))
             quantise(hg, h_q[i])
             if i + 2 < G:
                 quantise(ug, us_q[i + 2])
@@ -231,11 +266,13 @@ def tile_hybridsuperlayer_pb_kernel(tc, h_gelu, c_proj_U, c_proj_S, c_proj_V, c_
             if j >= LAG_B:
                 waiting.extend([(j - LAG_B, 1, m) for m in range(4)])
             for b in range(4):
-                stage1_bank(j, 1, b, b == 0 and j != 2)
+                stage1_bank(j, 1, b, b in VEC_B.get(j, (0,)))
+                if b == 0 and j > 0:
+                    quantise_w(j - 1, 1)
                 if taken[0] < len(waiting):
                     stage2_pass(*waiting[taken[0]])
                     taken[0] = taken[0] + 1
-            quantise_w(j, 1)
+        quantise_w(G - 1, 1)
         waiting.extend([(g, 1, m) for g in range(G - LAG_B, G - 2) for m in range(4)])
         waiting.extend([(g, 1, m) for m in range(4) for g in range(G - 2, G)])
         for item in waiting[taken[0] :]:

@@ -18,6 +18,7 @@ FLOPS = 2 * DFF * D * R + 2 * TOK * DFF * D
 VEC_A = {0: (1, 3)}
 VEC_B = {2: ()}
 LAST_PIECES = 1
+WARM = (5, 1, 1, 1, 2)
 NB = 4
 LAG_A = 2
 LAG_B = 3
@@ -224,16 +225,29 @@ def tile_hybridsuperlayer_pb_kernel(tc, h_gelu, c_proj_U, c_proj_S, c_proj_V, c_
             if g == G - 1:
                 finish(hf, m, LAST_PIECES if (hf == 1 and m == 3) else 1)
 
+        warm = keep.tile([P, 512], BF16, name="warm")
+        nc.vector.memset(warm[:], 0.0)
+        warm_bank = psum.tile([P, 512], F32, name="warm_bank", tag="acc3")
+
+        def keep_busy(n):
+            for k in range(n):
+                nc.tensor.matmul(out=warm_bank[:], lhsT=warm[:, 0:P], rhs=warm[:], start=True, stop=True)
+
+        keep_busy(WARM[0])
         ug0 = grouped_tile("usg")
         vg = grouped_tile("vg")
         bank_u = transpose_half(u_sb[0][:])
         scale_bank(bank_u, ug0[:, 0:1024])
+        keep_busy(WARM[1])
         bank_v = transpose_half(v_sb[0][:])
         copy_bank_words(bank_v, vg[:, 0:1024], False)
+        keep_busy(WARM[2])
         bank_u = transpose_half(u_sb[1][:])
         scale_bank(bank_u, ug0[:, 1024:2048])
+        keep_busy(WARM[3])
         bank_v = transpose_half(v_sb[1][:])
         copy_bank_words(bank_v, vg[:, 1024:2048], False)
+        keep_busy(WARM[4])
         quantise(vg, v_q[0], 0, 256)
         quantise(ug0, us_q[0])
         quantise(vg, v_q[0], 256, 512)

@@ -17,8 +17,6 @@ G = DFF // 512
 FLOPS = 2 * DFF * D * R + 2 * TOK * DFF * D
 VEC_A = {0: (1, 3)}
 VEC_B = {2: ()}
-LAST_PIECES = 1
-WARM = (5, 1, 1, 1, 2)
 NB = 4
 LAG_A = 2
 LAG_B = 3
@@ -39,7 +37,7 @@ def tile_hybridsuperlayer_pb_kernel(tc, h_gelu, c_proj_U, c_proj_S, c_proj_V, c_
 
         s4 = keep.tile([P, 2, 2], BF16, name="s4")
         with nc.allow_non_contiguous_dma(reason="512 singular values, two pairs to a partition"):
-            nc.sync.dma_start(out=s4[:], in_=c_proj_S.rearrange("(u p e) -> p u e", u=2, p=P, e=2))
+            nc.scalar.dma_start(out=s4[:], in_=c_proj_S.rearrange("(u p e) -> p u e", u=2, p=P, e=2))
         v_sb = [keep.tile([P, 1024], BF16, name="v_sb%d" % q) for q in range(4)]
         u_sb = [keep.tile([P, 1024], BF16, name="u_sb%d" % q) for q in range(2)] + [
             keep.tile([P, 2048], BF16, name="u_sb%d" % (g + 1)) for g in range(1, G)
@@ -166,6 +164,7 @@ def tile_hybridsuperlayer_pb_kernel(tc, h_gelu, c_proj_U, c_proj_S, c_proj_V, c_
         w_grouped = {}
         w_q = {}
         acc = {}
+        results = {}
 
         def stage1_bank(g, hf, db, on_vector):
             if db == 0:
@@ -194,60 +193,42 @@ def tile_hybridsuperlayer_pb_kernel(tc, h_gelu, c_proj_U, c_proj_S, c_proj_V, c_
             w_q[(g, hf)] = (codes, scales)
             quantise(w_grouped[(g, hf)], w_q[(g, hf)])
 
-        def finish(hf, m, pieces):
-            res = stage.tile([P, 512], F32, name="res", tag="res", bufs=4)
-            width = 512 // pieces
-            for c in range(pieces):
-                cols = slice(width * c, width * (c + 1))
-                nc.vector.tensor_tensor(
-                    out=res[:, cols],
-                    in0=acc[(hf, m)][:, cols],
-                    in1=bias_bc[:, 512 * hf + width * c : 512 * hf + width * (c + 1)],
-                    op=ADD,
-                )
-                nc.sync.dma_start(
-                    out=out_flat[128 * m : 128 * (m + 1), 512 * hf + width * c : 512 * hf + width * (c + 1)],
-                    in_=res[:, cols],
-                )
+        def finish(hf, m, lo, hi):
+            if lo == 0:
+                results[(hf, m)] = stage.tile([P, 512], F32, name="res", tag="res", bufs=4)
+            res = results[(hf, m)]
+            nc.vector.tensor_tensor(
+                out=res[:, lo:hi], in0=acc[(hf, m)][:, lo:hi], in1=bias_bc[:, 512 * hf + lo : 512 * hf + hi], op=ADD
+            )
+            nc.sync.dma_start(
+                out=out_flat[128 * m : 128 * (m + 1), 512 * hf + lo : 512 * hf + hi], in_=res[:, lo:hi]
+            )
 
-        def stage2_pass(g, hf, m):
-            if g == 0:
+        def stage2_pass(g, hf, m, lo=0, hi=512):
+            if g == 0 and lo == 0:
                 acc[(hf, m)] = psum.tile([P, 512], F32, name="acc%d" % m, tag="acc%d" % m)
             nc.tensor.matmul_mx(
-                out=acc[(hf, m)][:],
+                out=acc[(hf, m)][:, lo:hi],
                 lhsT=h_q[g][0][:, 128 * m : 128 * (m + 1)].bitcast(FP8X4),
                 lhsT_scale=h_q[g][1][:, 128 * m : 128 * (m + 1)],
-                rhs=w_q[(g, hf)][0][:].bitcast(FP8X4),
-                rhs_scale=w_q[(g, hf)][1][:],
+                rhs=w_q[(g, hf)][0][:, lo:hi].bitcast(FP8X4),
+                rhs_scale=w_q[(g, hf)][1][:, lo:hi],
                 start=(g == 0),
                 stop=(g == G - 1),
             )
             if g == G - 1:
-                finish(hf, m, LAST_PIECES if (hf == 1 and m == 3) else 1)
+                finish(hf, m, lo, hi)
 
-        warm = keep.tile([P, 512], BF16, name="warm")
-        nc.vector.memset(warm[:], 0.0)
-        warm_bank = psum.tile([P, 512], F32, name="warm_bank", tag="acc3")
-
-        def keep_busy(n):
-            for k in range(n):
-                nc.tensor.matmul(out=warm_bank[:], lhsT=warm[:, 0:P], rhs=warm[:], start=True, stop=True)
-
-        keep_busy(WARM[0])
         ug0 = grouped_tile("usg")
         vg = grouped_tile("vg")
         bank_u = transpose_half(u_sb[0][:])
         scale_bank(bank_u, ug0[:, 0:1024])
-        keep_busy(WARM[1])
         bank_v = transpose_half(v_sb[0][:])
         copy_bank_words(bank_v, vg[:, 0:1024], False)
-        keep_busy(WARM[2])
         bank_u = transpose_half(u_sb[1][:])
         scale_bank(bank_u, ug0[:, 1024:2048])
-        keep_busy(WARM[3])
         bank_v = transpose_half(v_sb[1][:])
         copy_bank_words(bank_v, vg[:, 1024:2048], False)
-        keep_busy(WARM[4])
         quantise(vg, v_q[0], 0, 256)
         quantise(ug0, us_q[0])
         quantise(vg, v_q[0], 256, 512)
@@ -278,7 +259,7 @@ def tile_hybridsuperlayer_pb_kernel(tc, h_gelu, c_proj_U, c_proj_S, c_proj_V, c_
         taken = [0]
         for j in range(G):
             if j >= LAG_B:
-                waiting.extend([(j - LAG_B, 1, m) for m in range(4)])
+                waiting.extend([(j - LAG_B, 1, m) for m in range(3)])
             for b in range(4):
                 stage1_bank(j, 1, b, b in VEC_B.get(j, (0,)))
                 if b == 0 and j > 0:
@@ -287,7 +268,10 @@ def tile_hybridsuperlayer_pb_kernel(tc, h_gelu, c_proj_U, c_proj_S, c_proj_V, c_
                     stage2_pass(*waiting[taken[0]])
                     taken[0] = taken[0] + 1
         quantise_w(G - 1, 1)
-        waiting.extend([(g, 1, m) for g in range(G - LAG_B, G - 2) for m in range(4)])
-        waiting.extend([(g, 1, m) for m in range(4) for g in range(G - 2, G)])
+        waiting.extend([(g, 1, m) for g in range(G - LAG_B, G - 2) for m in range(3)])
+        waiting.extend([(g, 1, 3, 0, 256) for g in range(G - 1)])
+        waiting.extend([(g, 1, m) for m in range(3) for g in range(G - 2, G)])
+        waiting.append((G - 1, 1, 3, 0, 256))
+        waiting.extend([(g, 1, 3, 256, 512) for g in range(G)])
         for item in waiting[taken[0] :]:
             stage2_pass(*item)

@@ -37,7 +37,7 @@ def tile_hybridsuperlayer_pb_kernel(tc, h_gelu, c_proj_U, c_proj_S, c_proj_V, c_
 
         s4 = keep.tile([P, 2, 2], BF16, name="s4")
         with nc.allow_non_contiguous_dma(reason="512 singular values, two pairs to a partition"):
-            nc.scalar.dma_start(out=s4[:], in_=c_proj_S.rearrange("(u p e) -> p u e", u=2, p=P, e=2))
+            nc.sync.dma_start(out=s4[:], in_=c_proj_S.rearrange("(u p e) -> p u e", u=2, p=P, e=2))
         v_sb = [keep.tile([P, 1024], BF16, name="v_sb%d" % q) for q in range(4)]
         u_sb = [keep.tile([P, 1024], BF16, name="u_sb%d" % q) for q in range(2)] + [
             keep.tile([P, 2048], BF16, name="u_sb%d" % (g + 1)) for g in range(1, G)
@@ -198,7 +198,7 @@ def tile_hybridsuperlayer_pb_kernel(tc, h_gelu, c_proj_U, c_proj_S, c_proj_V, c_
                 results[(hf, m)] = stage.tile([P, 512], F32, name="res", tag="res", bufs=4)
             res = results[(hf, m)]
             nc.vector.tensor_tensor(
-                out=res[:, lo:hi], in0=acc[(hf, m)][:, lo:hi], in1=bias_bc[:, 512 * hf + lo : 512 * hf + hi], op=ADD
+                out=res[:, lo:hi], in0=acc[(hf, m, lo)][:, lo:hi], in1=bias_bc[:, 512 * hf + lo : 512 * hf + hi], op=ADD
             )
             nc.sync.dma_start(
                 out=out_flat[128 * m : 128 * (m + 1), 512 * hf + lo : 512 * hf + hi], in_=res[:, lo:hi]
@@ -206,9 +206,11 @@ def tile_hybridsuperlayer_pb_kernel(tc, h_gelu, c_proj_U, c_proj_S, c_proj_V, c_
 
         def stage2_pass(g, hf, m, lo=0, hi=512):
             if g == 0 and lo == 0:
-                acc[(hf, m)] = psum.tile([P, 512], F32, name="acc%d" % m, tag="acc%d" % m)
+                acc[(hf, m, lo)] = psum.tile([P, 512], F32, name="acc%d" % m, tag="acc%d" % m)
+            elif g == 0:
+                acc[(hf, m, lo)] = next_bank()
             nc.tensor.matmul_mx(
-                out=acc[(hf, m)][:, lo:hi],
+                out=acc[(hf, m, lo)][:, lo:hi],
                 lhsT=h_q[g][0][:, 128 * m : 128 * (m + 1)].bitcast(FP8X4),
                 lhsT_scale=h_q[g][1][:, 128 * m : 128 * (m + 1)],
                 rhs=w_q[(g, hf)][0][:, lo:hi].bitcast(FP8X4),

@@ -15,11 +15,13 @@ P = 128
 TOK, D, DFF, R = 512, 1024, 4096, 512
 G = DFF // 512
 FLOPS = 2 * DFF * D * R + 2 * TOK * DFF * D
-VEC_A = {0: (1, 3)}
-VEC_B = {2: ()}
-NB = 4
-LAG_A = 2
-LAG_B = 3
+
+H_ROUND = {0: (0, 0), 1: (1, 0), 3: (2, 0), 4: (3, 0), 6: (0, 1), 7: (1, 1), 8: (2, 1), 9: (3, 1)}
+V2_ROUND = 5
+COPY_V = {0: (1, 3), 12: (0, 2), 13: (0, 2), 14: (0, 2), 15: (1, 3)}
+COPY_V_LATE = ()
+TAKE_EARLY = (0, 1, 0, 1)
+TAKE_LATE = (1, 1, 2, 1)
 
 
 def tile_hybridsuperlayer_pb_kernel(tc, h_gelu, c_proj_U, c_proj_S, c_proj_V, c_proj_bias, out):
@@ -38,11 +40,13 @@ def tile_hybridsuperlayer_pb_kernel(tc, h_gelu, c_proj_U, c_proj_S, c_proj_V, c_
         s4 = keep.tile([P, 2, 2], BF16, name="s4")
         with nc.allow_non_contiguous_dma(reason="512 singular values, two pairs to a partition"):
             nc.sync.dma_start(out=s4[:], in_=c_proj_S.rearrange("(u p e) -> p u e", u=2, p=P, e=2))
-        v_sb = [keep.tile([P, 1024], BF16, name="v_sb%d" % q) for q in range(4)]
+        v_sb = [keep.tile([P, 1024], BF16, name="v_sb%d" % q) for q in range(2)]
+        v2_sb = keep.tile([P, 2048], BF16, name="v2_sb", align_bytes=64)
         u_sb = [keep.tile([P, 1024], BF16, name="u_sb%d" % q) for q in range(2)] + [
             keep.tile([P, 2048], BF16, name="u_sb%d" % (g + 1)) for g in range(1, G)
         ]
-        h_sb = [keep.tile([P, 2048], BF16, name="h_sb%d" % g) for g in range(G)]
+        ha_sb = [keep.tile([P, 2048], BF16, name="ha_sb%d" % k) for k in range(4)]
+        hb_sb = [keep.tile([P, 2048], BF16, name="hb_sb%d" % k, align_bytes=64) for k in range(4)]
         bias_bc = keep.tile([P, D], BF16, name="bias_bc")
 
         def load_v(q):
@@ -63,24 +67,44 @@ def tile_hybridsuperlayer_pb_kernel(tc, h_gelu, c_proj_U, c_proj_S, c_proj_V, c_
                 in_=c_proj_U[512 * g : 512 * (g + 1), :].rearrange("(u p e) r -> p u (e r)", u=2, p=P, e=2),
             )
 
-        def load_h(g):
+        def load_ha(k):
             nc.sync.dma_start(
-                out=h_sb[g][:].rearrange("p (m k) -> p m k", m=4),
-                in_=h_flat[:, 512 * g : 512 * (g + 1)].rearrange("(m p) k -> p m k", p=P),
+                out=ha_sb[k][:].rearrange("p (m k) -> p m k", m=2),
+                in_=h_flat[0:256, 1024 * k : 1024 * (k + 1)].rearrange("(m p) k -> p m k", p=P),
             )
+
+        def load_split(dst, rows, col0):
+            for q in range(4):
+                for u in range(2):
+                    col = col0 + 256 * u + 64 * q
+                    nc.sync.dma_start(
+                        out=dst[32 * q + u : 32 * q + 32 : 2, :].rearrange("r (c w) -> r c w", w=64),
+                        in_=rows[:, col : col + 64].rearrange("(c r) w -> r c w", r=16),
+                    )
+
+        def load_hb(k):
+            for c in range(2):
+                load_split(hb_sb[k][:, 1024 * c : 1024 * (c + 1)], h_flat[256:512, :], 512 * (2 * k + c))
 
         load_u_half(0)
         load_v(0)
         load_u_half(1)
         load_v(1)
         load_u(1)
-        for g in range(G):
-            load_h(g)
-            if g + 2 < G:
-                load_u(g + 2)
-        load_v(2)
-        load_v(3)
+        load_ha(0)
+        load_u(2)
+        load_u(3)
+        load_ha(1)
+        load_u(4)
+        load_u(5)
+        load_ha(2)
+        load_split(v2_sb, c_proj_V[512:1024, :], 0)
+        load_u(6)
+        load_u(7)
+        load_ha(3)
         nc.sync.dma_start(out=bias_bc[:], in_=c_proj_bias.partition_broadcast(P))
+        for k in range(4):
+            load_hb(k)
 
         def halves(tile_ap):
             return [tile_ap[:, 0:1024], tile_ap[:, 1024:2048]]
@@ -96,37 +120,37 @@ def tile_hybridsuperlayer_pb_kernel(tc, h_gelu, c_proj_U, c_proj_S, c_proj_V, c_
             return codes, scales
 
         us_q = [codes_and_scales("us%d" % g) for g in range(G)]
-        h_q = [codes_and_scales("h%d" % g) for g in range(G)]
+        h_q = [[codes_and_scales("h%d_%d" % (k, z)) for z in range(2)] for k in range(4)]
         v_q = [codes_and_scales("v%d" % hf) for hf in range(2)]
 
-        count = [0]
-        banks_in_use = [8]
+        bank_names = ["w0", "w1", "w2", "w3", "acc3", "acc2", "acc1", "acc0"]
+        count = [0, 8]
 
         def next_bank():
-            b = count[0] % banks_in_use[0]
+            name = bank_names[count[0] % count[1]]
             count[0] = count[0] + 1
-            if b >= NB:
-                return psum.tile([P, 512], F32, name="spare%d" % (b - NB), tag="acc%d" % (b - NB))
-            return psum.tile([P, 512], F32, name="w%d" % b, tag="w%d" % b)
+            return psum.tile([P, 512], F32, name=name, tag=name)
 
         def quantise(grouped, pair, lo=0, hi=512):
             nc.vector.quantize_mx(
                 out=pair[0][:, lo:hi].bitcast(FP8X4), scales=pair[1][:, lo:hi], in_=grouped[:, 4 * lo : 4 * hi]
             )
 
-        def transpose_half(src):
-            words = src.bitcast(F32)
+        def transpose_rows(words, pitch):
             bank = next_bank()
             for j in range(2):
                 for u in range(2):
                     nc.tensor.transpose(
                         bank[:, 256 * u + 128 * j : 256 * u + 128 * j + 128],
-                        words[:, 256 * j + 128 * u : 256 * j + 128 * u + 128],
+                        words[:, pitch * j + 128 * u : pitch * j + 128 * u + 128],
                         ident[:],
                     )
             return bank
 
-        def copy_bank_words(bank, dst_bf16, on_vector):
+        def transpose_half(src):
+            return transpose_rows(src.bitcast(F32), 256)
+
+        def copy_bank_words(bank, dst_bf16, on_vector=False):
             dst = dst_bf16.bitcast(F32).rearrange("p (c u) -> p c u", u=2)
             src = bank[:].rearrange("p (u c) -> p c u", u=2)
             if on_vector:
@@ -154,17 +178,22 @@ def tile_hybridsuperlayer_pb_kernel(tc, h_gelu, c_proj_U, c_proj_S, c_proj_V, c_
                 scale_bank(banks[half], grouped[:, 1024 * half : 1024 * (half + 1)])
             return grouped
 
-        def prepare_words(sources, tag, on_vector):
+        def prepare_ha(k):
+            grouped = grouped_tile("hg")
+            words = ha_sb[k][:].bitcast(F32)
+            banks = [transpose_rows(words[:, 256 * c : 1024], 512) for c in range(2)]
+            for c in range(2):
+                copy_bank_words(banks[c], grouped[:, 1024 * c : 1024 * (c + 1)])
+            return grouped
+
+        def prepare_blocks(src, tag):
             grouped = grouped_tile(tag)
-            banks = [transpose_half(src) for src in sources]
-            for half in range(2):
-                copy_bank_words(banks[half], grouped[:, 1024 * half : 1024 * (half + 1)], on_vector[half])
+            nc.vector.transpose(out=grouped[:].bitcast(F32), in_=src[:].bitcast(F32))
             return grouped
 
         w_grouped = {}
         w_q = {}
         acc = {}
-        results = {}
 
         def stage1_bank(g, hf, db, on_vector):
             if db == 0:
@@ -188,15 +217,11 @@ def tile_hybridsuperlayer_pb_kernel(tc, h_gelu, c_proj_U, c_proj_S, c_proj_V, c_
                 nc.scalar.copy(out=dst, in_=src)
 
         def quantise_w(g, hf):
-            codes = keep.tile([P, 512], U32, name="w%d_c" % g, tag="w%d_c" % g, align_bytes=64)
-            scales = keep.tile([P, 512], U8, name="w%d_s" % g, tag="w%d_s" % g, align_bytes=64)
-            w_q[(g, hf)] = (codes, scales)
+            w_q[(g, hf)] = codes_and_scales("w%d_%d" % (g, hf))
             quantise(w_grouped[(g, hf)], w_q[(g, hf)])
 
         def finish(hf, m, lo, hi):
-            if lo == 0:
-                results[(hf, m)] = stage.tile([P, 512], F32, name="res", tag="res", bufs=4)
-            res = results[(hf, m)]
+            res = stage.tile([P, 512], F32, name="res", tag="res", bufs=4)
             nc.vector.tensor_tensor(
                 out=res[:, lo:hi], in0=acc[(hf, m, lo)][:, lo:hi], in1=bias_bc[:, 512 * hf + lo : 512 * hf + hi], op=ADD
             )
@@ -209,10 +234,12 @@ def tile_hybridsuperlayer_pb_kernel(tc, h_gelu, c_proj_U, c_proj_S, c_proj_V, c_
                 acc[(hf, m, lo)] = psum.tile([P, 512], F32, name="acc%d" % m, tag="acc%d" % m)
             elif g == 0:
                 acc[(hf, m, lo)] = next_bank()
+            codes, scales = h_q[g // 2][m // 2]
+            col = 256 * (g % 2) + 128 * (m % 2)
             nc.tensor.matmul_mx(
                 out=acc[(hf, m, lo)][:, lo:hi],
-                lhsT=h_q[g][0][:, 128 * m : 128 * (m + 1)].bitcast(FP8X4),
-                lhsT_scale=h_q[g][1][:, 128 * m : 128 * (m + 1)],
+                lhsT=codes[:, col : col + 128].bitcast(FP8X4),
+                lhsT_scale=scales[:, col : col + 128],
                 rhs=w_q[(g, hf)][0][:, lo:hi].bitcast(FP8X4),
                 rhs_scale=w_q[(g, hf)][1][:, lo:hi],
                 start=(g == 0),
@@ -226,54 +253,73 @@ def tile_hybridsuperlayer_pb_kernel(tc, h_gelu, c_proj_U, c_proj_S, c_proj_V, c_
         bank_u = transpose_half(u_sb[0][:])
         scale_bank(bank_u, ug0[:, 0:1024])
         bank_v = transpose_half(v_sb[0][:])
-        copy_bank_words(bank_v, vg[:, 0:1024], False)
+        copy_bank_words(bank_v, vg[:, 0:1024])
         bank_u = transpose_half(u_sb[1][:])
         scale_bank(bank_u, ug0[:, 1024:2048])
         bank_v = transpose_half(v_sb[1][:])
-        copy_bank_words(bank_v, vg[:, 1024:2048], False)
+        copy_bank_words(bank_v, vg[:, 1024:2048])
         quantise(vg, v_q[0], 0, 256)
         quantise(ug0, us_q[0])
         quantise(vg, v_q[0], 256, 512)
         ug1 = prepare_u(1)
         quantise(ug1, us_q[1])
 
-        for i in range(G):
-            if i == LAG_A:
-                banks_in_use[0] = NB
-                count[0] = 0
-            for b in range(4):
-                stage1_bank(i, 0, b, b in VEC_A.get(i, ()))
-                if i >= LAG_A:
-                    stage2_pass(i - LAG_A, 0, (b + 2) % 4)
-            quantise_w(i, 0)
-            hg = prepare_words(halves(h_sb[i]), "hg", (False, False))
-            if i + 2 < G:
-                ug = prepare_u(i + 2)
-            elif i + 2 == G:
-                vg = prepare_words([v_sb[2][:], v_sb[3][:]], "vg", (True, True))
-            quantise(hg, h_q[i])
-            if i + 2 < G:
-                quantise(ug, us_q[i + 2])
-            elif i + 2 == G:
-                quantise(vg, v_q[1])
+        order = [(g, 0) for g in range(G)] + [(g, 1) for g in range(G)]
+        slot = {}
+        for r, (g, hf) in enumerate(order):
+            slot[(g, hf)] = r
+        h_ready = {}
+        for r in H_ROUND:
+            h_ready[H_ROUND[r]] = r
 
-        waiting = [(g, 0, m) for g in range(G - LAG_A, G) for m in range(4)]
-        taken = [0]
-        for j in range(G):
-            if j >= LAG_B:
-                waiting.extend([(j - LAG_B, 1, m) for m in range(3)])
+        def is_ready(item, r):
+            g, hf, m = item[0], item[1], item[2]
+            return r >= slot[(g, hf)] + 2 and r >= h_ready[(g // 2, m // 2)] + 1
+
+        passes = [(g, 0, m) for g in range(G) for m in range(2)]
+        first = [(g, 0, m) for g in range(G) for m in range(2, 4)]
+        second = [(g, 1, m) for g in range(G - 2) for m in range(2)]
+        third = [(g, 1, m) for g in range(G - 2) for m in range(2, 4)]
+        passes = passes[0:14] + first[0:4] + passes[14:16] + first[4:8]
+        passes += first[8:12] + second[0:2] + first[12:16] + second[2:4]
+        for k in range(2, G - 2):
+            passes += second[2 * k : 2 * k + 2] + third[4 * k - 8 : 4 * k - 4]
+        passes += third[4 * (G - 4) : ]
+        passes += [(g, 1, m) for m in range(3) for g in range(G - 2, G)]
+        passes += [(g, 1, 3) for g in range(G - 2, G)]
+        assert len(passes) == 64
+
+        def take(n, r):
+            while n > 0 and passes and is_ready(passes[0], r):
+                stage2_pass(*passes[0])
+                passes.remove(passes[0])
+                n = n - 1
+
+        for r, (g, hf) in enumerate(order):
+            if r == 2:
+                count[1] = 6
+                count[0] = 0
+            if r == 7:
+                count[1] = 4
+                count[0] = 0
+            on_v = COPY_V.get(r, () if hf == 0 else COPY_V_LATE)
             for b in range(4):
-                stage1_bank(j, 1, b, b in VEC_B.get(j, (0,)))
-                if b == 0 and j > 0:
-                    quantise_w(j - 1, 1)
-                if taken[0] < len(waiting):
-                    stage2_pass(*waiting[taken[0]])
-                    taken[0] = taken[0] + 1
+                stage1_bank(g, hf, b, b in on_v)
+                if hf == 1 and b == 0 and g > 0:
+                    quantise_w(g - 1, 1)
+                take((TAKE_EARLY if hf == 0 else TAKE_LATE)[b], r)
+            late = []
+            if r in H_ROUND and H_ROUND[r][1] == 1:
+                late.append((prepare_blocks(hb_sb[H_ROUND[r][0]], "hg"), h_q[H_ROUND[r][0]][1]))
+            if r == V2_ROUND:
+                late.append((prepare_blocks(v2_sb, "vg"), v_q[1]))
+            if r + 2 < G:
+                late.append((prepare_u(r + 2), us_q[r + 2]))
+            if hf == 0:
+                quantise_w(g, 0)
+            if r in H_ROUND and H_ROUND[r][1] == 0:
+                late.append((prepare_ha(H_ROUND[r][0]), h_q[H_ROUND[r][0]][0]))
+            for grouped, codes in late:
+                quantise(grouped, codes)
         quantise_w(G - 1, 1)
-        waiting.extend([(g, 1, m) for g in range(G - LAG_B, G - 2) for m in range(3)])
-        waiting.extend([(g, 1, 3, 0, 256) for g in range(G - 1)])
-        waiting.extend([(g, 1, m) for m in range(3) for g in range(G - 2, G)])
-        waiting.append((G - 1, 1, 3, 0, 256))
-        waiting.extend([(g, 1, 3, 256, 512) for g in range(G)])
-        for item in waiting[taken[0] :]:
-            stage2_pass(*item)
+        take(len(passes), 99)

@@ -16,9 +16,10 @@ TOK, D, DFF, R = 512, 1024, 4096, 512
 G = DFF // 512
 FLOPS = 2 * DFF * D * R + 2 * TOK * DFF * D
 
-H_ROUND = {0: (0, 0), 1: (1, 0), 3: (2, 0), 4: (3, 0), 6: (0, 1), 7: (1, 1), 8: (2, 1), 9: (3, 1)}
-V2_ROUND = 5
-COPY_V = {0: (1, 3), 12: (0, 2), 13: (0, 2), 14: (0, 2), 15: (1, 3)}
+H_ROUND = {0: [(0, 0)], 1: [(1, 0)], 3: [(2, 0)], 4: [(3, 0)], 5: [(0, 1)], 6: [(1, 1)], 8: [(2, 1)], 10: [(3, 1)]}
+BLOCKS = (2, 3)
+V2_ROUND = 6
+COPY_V = {0: (3,), 12: (0, 2), 13: (0, 2), 14: (0, 2), 15: (1, 3)}
 COPY_V_LATE = ()
 TAKE_EARLY = (0, 1, 0, 1)
 TAKE_LATE = (1, 1, 2, 1)
@@ -45,8 +46,10 @@ def tile_hybridsuperlayer_pb_kernel(tc, h_gelu, c_proj_U, c_proj_S, c_proj_V, c_
         u_sb = [keep.tile([P, 1024], BF16, name="u_sb%d" % q) for q in range(2)] + [
             keep.tile([P, 2048], BF16, name="u_sb%d" % (g + 1)) for g in range(1, G)
         ]
-        ha_sb = [keep.tile([P, 2048], BF16, name="ha_sb%d" % k) for k in range(4)]
-        hb_sb = [keep.tile([P, 2048], BF16, name="hb_sb%d" % k, align_bytes=64) for k in range(4)]
+        h_sb = {}
+        for k in range(4):
+            for z in range(2):
+                h_sb[(k, z)] = keep.tile([P, 2048], BF16, name="h_sb%d_%d" % (k, z), align_bytes=64)
         bias_bc = keep.tile([P, D], BF16, name="bias_bc")
 
         def load_v(q):
@@ -67,10 +70,10 @@ def tile_hybridsuperlayer_pb_kernel(tc, h_gelu, c_proj_U, c_proj_S, c_proj_V, c_
                 in_=c_proj_U[512 * g : 512 * (g + 1), :].rearrange("(u p e) r -> p u (e r)", u=2, p=P, e=2),
             )
 
-        def load_ha(k):
+        def load_h(k, z):
             nc.sync.dma_start(
-                out=ha_sb[k][:].rearrange("p (m k) -> p m k", m=2),
-                in_=h_flat[0:256, 1024 * k : 1024 * (k + 1)].rearrange("(m p) k -> p m k", p=P),
+                out=h_sb[(k, z)][:].rearrange("p (m k) -> p m k", m=2),
+                in_=h_flat[256 * z : 256 * (z + 1), 1024 * k : 1024 * (k + 1)].rearrange("(m p) k -> p m k", p=P),
             )
 
         def load_split(dst, rows, col0):
@@ -82,29 +85,31 @@ def tile_hybridsuperlayer_pb_kernel(tc, h_gelu, c_proj_U, c_proj_S, c_proj_V, c_
                         in_=rows[:, col : col + 64].rearrange("(c r) w -> r c w", r=16),
                     )
 
-        def load_hb(k):
+        def load_blocks(k):
             for c in range(2):
-                load_split(hb_sb[k][:, 1024 * c : 1024 * (c + 1)], h_flat[256:512, :], 512 * (2 * k + c))
+                load_split(h_sb[(k, 1)][:, 1024 * c : 1024 * (c + 1)], h_flat[256:512, :], 512 * (2 * k + c))
 
         load_u_half(0)
         load_v(0)
         load_u_half(1)
         load_v(1)
         load_u(1)
-        load_ha(0)
+        load_h(0, 0)
         load_u(2)
+        load_h(1, 0)
         load_u(3)
-        load_ha(1)
         load_u(4)
+        load_h(2, 0)
         load_u(5)
-        load_ha(2)
-        load_split(v2_sb, c_proj_V[512:1024, :], 0)
+        load_h(3, 0)
         load_u(6)
+        load_h(0, 1)
         load_u(7)
-        load_ha(3)
+        load_h(1, 1)
+        load_split(v2_sb, c_proj_V[512:1024, :], 0)
         nc.sync.dma_start(out=bias_bc[:], in_=c_proj_bias.partition_broadcast(P))
-        for k in range(4):
-            load_hb(k)
+        load_blocks(2)
+        load_blocks(3)
 
         def halves(tile_ap):
             return [tile_ap[:, 0:1024], tile_ap[:, 1024:2048]]
@@ -120,7 +125,10 @@ def tile_hybridsuperlayer_pb_kernel(tc, h_gelu, c_proj_U, c_proj_S, c_proj_V, c_
             return codes, scales
 
         us_q = [codes_and_scales("us%d" % g) for g in range(G)]
-        h_q = [[codes_and_scales("h%d_%d" % (k, z)) for z in range(2)] for k in range(4)]
+        h_q = {}
+        for k in range(4):
+            for z in range(2):
+                h_q[(k, z)] = codes_and_scales("h%d_%d" % (k, z))
         v_q = [codes_and_scales("v%d" % hf) for hf in range(2)]
 
         bank_names = ["w0", "w1", "w2", "w3", "acc3", "acc2", "acc1", "acc0"]
@@ -178,9 +186,9 @@ def tile_hybridsuperlayer_pb_kernel(tc, h_gelu, c_proj_U, c_proj_S, c_proj_V, c_
                 scale_bank(banks[half], grouped[:, 1024 * half : 1024 * (half + 1)])
             return grouped
 
-        def prepare_ha(k):
+        def prepare_h(k, z):
             grouped = grouped_tile("hg")
-            words = ha_sb[k][:].bitcast(F32)
+            words = h_sb[(k, z)][:].bitcast(F32)
             banks = [transpose_rows(words[:, 256 * c : 1024], 512) for c in range(2)]
             for c in range(2):
                 copy_bank_words(banks[c], grouped[:, 1024 * c : 1024 * (c + 1)])
@@ -234,7 +242,7 @@ def tile_hybridsuperlayer_pb_kernel(tc, h_gelu, c_proj_U, c_proj_S, c_proj_V, c_
                 acc[(hf, m, lo)] = psum.tile([P, 512], F32, name="acc%d" % m, tag="acc%d" % m)
             elif g == 0:
                 acc[(hf, m, lo)] = next_bank()
-            codes, scales = h_q[g // 2][m // 2]
+            codes, scales = h_q[(g // 2, m // 2)]
             col = 256 * (g % 2) + 128 * (m % 2)
             nc.tensor.matmul_mx(
                 out=acc[(hf, m, lo)][:, lo:hi],
@@ -270,7 +278,8 @@ def tile_hybridsuperlayer_pb_kernel(tc, h_gelu, c_proj_U, c_proj_S, c_proj_V, c_
             slot[(g, hf)] = r
         h_ready = {}
         for r in H_ROUND:
-            h_ready[H_ROUND[r]] = r
+            for unit in H_ROUND[r]:
+                h_ready[unit] = r
 
         def is_ready(item, r):
             g, hf, m = item[0], item[1], item[2]
@@ -309,16 +318,21 @@ def tile_hybridsuperlayer_pb_kernel(tc, h_gelu, c_proj_U, c_proj_S, c_proj_V, c_
                     quantise_w(g - 1, 1)
                 take((TAKE_EARLY if hf == 0 else TAKE_LATE)[b], r)
             late = []
-            if r in H_ROUND and H_ROUND[r][1] == 1:
-                late.append((prepare_blocks(hb_sb[H_ROUND[r][0]], "hg"), h_q[H_ROUND[r][0]][1]))
+            units = H_ROUND.get(r, ())
+            for k, z in units:
+                if z == 1 and k in BLOCKS:
+                    late.append((prepare_blocks(h_sb[(k, z)], "hg"), h_q[(k, z)]))
             if r == V2_ROUND:
                 late.append((prepare_blocks(v2_sb, "vg"), v_q[1]))
             if r + 2 < G:
-                late.append((prepare_u(r + 2), us_q[r + 2]))
+                ug = prepare_u(r + 2)
             if hf == 0:
                 quantise_w(g, 0)
-            if r in H_ROUND and H_ROUND[r][1] == 0:
-                late.append((prepare_ha(H_ROUND[r][0]), h_q[H_ROUND[r][0]][0]))
+            for k, z in units:
+                if z == 0 or k not in BLOCKS:
+                    late.append((prepare_h(k, z), h_q[(k, z)]))
+            if r + 2 < G:
+                quantise(ug, us_q[r + 2])
             for grouped, codes in late:
                 quantise(grouped, codes)
         quantise_w(G - 1, 1)

@@ -16,13 +16,13 @@ TOK, D, DFF, R = 512, 1024, 4096, 512
 G = DFF // 512
 FLOPS = 2 * DFF * D * R + 2 * TOK * DFF * D
 
-H_ROUND = {0: [(0, 0)], 1: [(1, 0)], 3: [(2, 0)], 4: [(3, 0)], 5: [(0, 1)], 6: [(1, 1)], 8: [(2, 1)], 10: [(3, 1)]}
+H_ROUND = {0: [(0, 0)], 2: [(1, 0)], 3: [(2, 0)], 4: [(3, 0)], 5: [(0, 1)], 6: [(1, 1)], 10: [(2, 1)], 12: [(3, 1)]}
 BLOCKS = (2, 3)
 V2_ROUND = 6
-COPY_V = {0: (3,), 12: (0, 2), 13: (0, 2), 14: (0, 2), 15: (1, 3)}
-COPY_V_LATE = ()
+COPY_V = {0: (3,), 7: (3,), 8: (), 9: (), 15: (1, 3)}
+COPY_V_LATE = (1,)
 TAKE_EARLY = (0, 1, 0, 1)
-TAKE_LATE = (1, 1, 2, 1)
+TAKE_LATE = (1, 1, 1, 1)
 
 
 def tile_hybridsuperlayer_pb_kernel(tc, h_gelu, c_proj_U, c_proj_S, c_proj_V, c_proj_bias, out):
@@ -229,7 +229,7 @@ def tile_hybridsuperlayer_pb_kernel(tc, h_gelu, c_proj_U, c_proj_S, c_proj_V, c_
             quantise(w_grouped[(g, hf)], w_q[(g, hf)])
 
         def finish(hf, m, lo, hi):
-            res = stage.tile([P, 512], F32, name="res", tag="res", bufs=4)
+            res = stage.tile([P, 512], F32, name="res", tag="res", bufs=6)
             nc.vector.tensor_tensor(
                 out=res[:, lo:hi], in0=acc[(hf, m, lo)][:, lo:hi], in1=bias_bc[:, 512 * hf + lo : 512 * hf + hi], op=ADD
             )
@@ -262,12 +262,13 @@ def tile_hybridsuperlayer_pb_kernel(tc, h_gelu, c_proj_U, c_proj_S, c_proj_V, c_
         scale_bank(bank_u, ug0[:, 0:1024])
         bank_v = transpose_half(v_sb[0][:])
         copy_bank_words(bank_v, vg[:, 0:1024])
+        quantise(ug0, us_q[0], 0, 256)
         bank_u = transpose_half(u_sb[1][:])
         scale_bank(bank_u, ug0[:, 1024:2048])
         bank_v = transpose_half(v_sb[1][:])
         copy_bank_words(bank_v, vg[:, 1024:2048])
         quantise(vg, v_q[0], 0, 256)
-        quantise(ug0, us_q[0])
+        quantise(ug0, us_q[0], 256, 512)
         quantise(vg, v_q[0], 256, 512)
         ug1 = prepare_u(1)
         quantise(ug1, us_q[1])
@@ -287,16 +288,13 @@ def tile_hybridsuperlayer_pb_kernel(tc, h_gelu, c_proj_U, c_proj_S, c_proj_V, c_
 
         passes = [(g, 0, m) for g in range(G) for m in range(2)]
         first = [(g, 0, m) for g in range(G) for m in range(2, 4)]
-        second = [(g, 1, m) for g in range(G - 2) for m in range(2)]
-        third = [(g, 1, m) for g in range(G - 2) for m in range(2, 4)]
-        passes = passes[0:14] + first[0:4] + passes[14:16] + first[4:8]
-        passes += first[8:12] + second[0:2] + first[12:16] + second[2:4]
-        for k in range(2, G - 2):
-            passes += second[2 * k : 2 * k + 2] + third[4 * k - 8 : 4 * k - 4]
-        passes += third[4 * (G - 4) : ]
-        passes += [(g, 1, m) for m in range(3) for g in range(G - 2, G)]
-        passes += [(g, 1, 3) for g in range(G - 2, G)]
-        assert len(passes) == 64
+        second = [(g, 1, m) for g in range(G) for m in range(2)]
+        passes = passes[0:14] + first[0:2] + passes[14:16] + first[2:4]
+        for k in range(2, G):
+            passes += first[2 * k : 2 * k + 2] + second[2 * k - 4 : 2 * k - 2]
+        passes += second[12:14] + [(g, 1, 2) for g in range(G - 1)] + second[14:16] + [(G - 1, 1, 2)]
+        passes += [(g, 1, 3, 0, 256) for g in range(G)] + [(g, 1, 3, 256, 512) for g in range(G)]
+        assert len(passes) == 72
 
         def take(n, r):
             while n > 0 and passes and is_ready(passes[0], r):
@@ -307,7 +305,7 @@ def tile_hybridsuperlayer_pb_kernel(tc, h_gelu, c_proj_U, c_proj_S, c_proj_V, c_
         for r, (g, hf) in enumerate(order):
             if r == 2:
                 count[1] = 6
-                count[0] = 0
+                count[0] = 4
             if r == 7:
                 count[1] = 4
                 count[0] = 0

@@ -16,10 +16,10 @@ TOK, D, DFF, R = 512, 1024, 4096, 512
 G = DFF // 512
 FLOPS = 2 * DFF * D * R + 2 * TOK * DFF * D
 
-H_ROUND = {0: [(0, 0)], 2: [(1, 0)], 3: [(2, 0)], 4: [(3, 0)], 5: [(0, 1)], 6: [(1, 1)], 10: [(2, 1)], 12: [(3, 1)]}
-BLOCKS = (2, 3)
-V2_ROUND = 6
-COPY_V = {0: (3,), 7: (3,), 8: (), 9: (), 15: (1, 3)}
+H_ROUND = {0: [(0, 0)], 2: [(1, 0)], 3: [(2, 0)], 4: [(3, 0)], 5: [(0, 1)], 8: [(1, 1)], 11: [(2, 1)], 13: [(3, 1)]}
+BLOCKS = (1, 2, 3)
+V2_ROUND = 5
+COPY_V = {3: (3,), 4: (3,), 7: (3,), 8: (), 9: (), 15: (1, 3)}
 COPY_V_LATE = (1,)
 TAKE_EARLY = (0, 1, 0, 1)
 TAKE_LATE = (1, 1, 1, 1)
@@ -41,8 +41,7 @@ def tile_hybridsuperlayer_pb_kernel(tc, h_gelu, c_proj_U, c_proj_S, c_proj_V, c_
         s4 = keep.tile([P, 2, 2], BF16, name="s4")
         with nc.allow_non_contiguous_dma(reason="512 singular values, two pairs to a partition"):
             nc.sync.dma_start(out=s4[:], in_=c_proj_S.rearrange("(u p e) -> p u e", u=2, p=P, e=2))
-        v_sb = [keep.tile([P, 1024], BF16, name="v_sb%d" % q) for q in range(2)]
-        v2_sb = keep.tile([P, 2048], BF16, name="v2_sb", align_bytes=64)
+        v_sb = [keep.tile([P, 1024], BF16, name="v_sb%d" % q) for q in range(4)]
         u_sb = [keep.tile([P, 1024], BF16, name="u_sb%d" % q) for q in range(2)] + [
             keep.tile([P, 2048], BF16, name="u_sb%d" % (g + 1)) for g in range(1, G)
         ]
@@ -103,11 +102,12 @@ def tile_hybridsuperlayer_pb_kernel(tc, h_gelu, c_proj_U, c_proj_S, c_proj_V, c_
         load_u(5)
         load_h(3, 0)
         load_u(6)
-        load_h(0, 1)
+        load_v(2)
+        load_v(3)
         load_u(7)
-        load_h(1, 1)
-        load_split(v2_sb, c_proj_V[512:1024, :], 0)
+        load_h(0, 1)
         nc.sync.dma_start(out=bias_bc[:], in_=c_proj_bias.partition_broadcast(P))
+        load_blocks(1)
         load_blocks(2)
         load_blocks(3)
 
@@ -192,6 +192,13 @@ def tile_hybridsuperlayer_pb_kernel(tc, h_gelu, c_proj_U, c_proj_S, c_proj_V, c_
             banks = [transpose_rows(words[:, 256 * c : 1024], 512) for c in range(2)]
             for c in range(2):
                 copy_bank_words(banks[c], grouped[:, 1024 * c : 1024 * (c + 1)])
+            return grouped
+
+        def prepare_v2():
+            grouped = grouped_tile("vg")
+            banks = [transpose_half(v_sb[q][:]) for q in range(2, 4)]
+            for half in range(2):
+                copy_bank_words(banks[half], grouped[:, 1024 * half : 1024 * (half + 1)], True)
             return grouped
 
         def prepare_blocks(src, tag):
@@ -291,7 +298,7 @@ def tile_hybridsuperlayer_pb_kernel(tc, h_gelu, c_proj_U, c_proj_S, c_proj_V, c_
         second = [(g, 1, m) for g in range(G) for m in range(2)]
         passes = passes[0:14] + first[0:2] + passes[14:16] + first[2:4]
         for k in range(2, G):
-            passes += first[2 * k : 2 * k + 2] + second[2 * k - 4 : 2 * k - 2]
+            passes += second[2 * k - 4 : 2 * k - 2] + first[2 * k : 2 * k + 2]
         passes += second[12:14] + [(g, 1, 2) for g in range(G - 1)] + second[14:16] + [(G - 1, 1, 2)]
         passes += [(g, 1, 3, 0, 256) for g in range(G)] + [(g, 1, 3, 256, 512) for g in range(G)]
         assert len(passes) == 72
@@ -320,8 +327,6 @@ def tile_hybridsuperlayer_pb_kernel(tc, h_gelu, c_proj_U, c_proj_S, c_proj_V, c_
             for k, z in units:
                 if z == 1 and k in BLOCKS:
                     late.append((prepare_blocks(h_sb[(k, z)], "hg"), h_q[(k, z)]))
-            if r == V2_ROUND:
-                late.append((prepare_blocks(v2_sb, "vg"), v_q[1]))
             if r + 2 < G:
                 ug = prepare_u(r + 2)
             if hf == 0:
@@ -329,6 +334,8 @@ def tile_hybridsuperlayer_pb_kernel(tc, h_gelu, c_proj_U, c_proj_S, c_proj_V, c_
             for k, z in units:
                 if z == 0 or k not in BLOCKS:
                     late.append((prepare_h(k, z), h_q[(k, z)]))
+            if r == V2_ROUND:
+                late.append((prepare_v2(), v_q[1]))
             if r + 2 < G:
                 quantise(ug, us_q[r + 2])
             for grouped, codes in late:

@@ -16,10 +16,10 @@ TOK, D, DFF, R = 512, 1024, 4096, 512
 G = DFF // 512
 FLOPS = 2 * DFF * D * R + 2 * TOK * DFF * D
 
-H_ROUND = {0: [(0, 0)], 2: [(1, 0)], 3: [(2, 0)], 4: [(3, 0)], 5: [(0, 1)], 8: [(1, 1)], 11: [(2, 1)], 13: [(3, 1)]}
+H_ROUND = {0: [(0, 0)], 2: [(1, 0)], 4: [(2, 0)], 5: [(3, 0), (0, 1)], 8: [(1, 1)], 10: [(2, 1)], 12: [(3, 1)]}
 BLOCKS = (1, 2, 3)
 V2_ROUND = 5
-COPY_V = {3: (3,), 4: (3,), 7: (3,), 8: (), 9: (), 15: (1, 3)}
+COPY_V = {3: (3,), 4: (3,), 7: (3,), 8: (), 9: (), 10: (), 12: (), 15: (1, 3)}
 COPY_V_LATE = (1,)
 TAKE_EARLY = (0, 1, 0, 1)
 TAKE_LATE = (1, 1, 1, 1)
@@ -298,7 +298,7 @@ def tile_hybridsuperlayer_pb_kernel(tc, h_gelu, c_proj_U, c_proj_S, c_proj_V, c_
         second = [(g, 1, m) for g in range(G) for m in range(2)]
         passes = passes[0:14] + first[0:2] + passes[14:16] + first[2:4]
         for k in range(2, G):
-            passes += second[2 * k - 4 : 2 * k - 2] + first[2 * k : 2 * k + 2]
+            passes += first[2 * k : 2 * k + 2] + second[2 * k - 4 : 2 * k - 2]
         passes += second[12:14] + [(g, 1, 2) for g in range(G - 1)] + second[14:16] + [(G - 1, 1, 2)]
         passes += [(g, 1, 3, 0, 256) for g in range(G)] + [(g, 1, 3, 256, 512) for g in range(G)]
         assert len(passes) == 72

@@ -39,8 +39,6 @@ def tile_hybridsuperlayer_pb_kernel(tc, h_gelu, c_proj_U, c_proj_S, c_proj_V, c_
         make_identity(nc, ident[:])
 
         s4 = keep.tile([P, 2, 2], BF16, name="s4")
-        with nc.allow_non_contiguous_dma(reason="512 singular values, two pairs to a partition"):
-            nc.sync.dma_start(out=s4[:], in_=c_proj_S.rearrange("(u p e) -> p u e", u=2, p=P, e=2))
         v_sb = [keep.tile([P, 1024], BF16, name="v_sb%d" % q) for q in range(4)]
         u_sb = [keep.tile([P, 1024], BF16, name="u_sb%d" % q) for q in range(2)] + [
             keep.tile([P, 2048], BF16, name="u_sb%d" % (g + 1)) for g in range(1, G)
@@ -50,6 +48,10 @@ def tile_hybridsuperlayer_pb_kernel(tc, h_gelu, c_proj_U, c_proj_S, c_proj_V, c_
             for z in range(2):
                 h_sb[(k, z)] = keep.tile([P, 2048], BF16, name="h_sb%d_%d" % (k, z), align_bytes=64)
         bias_bc = keep.tile([P, D], BF16, name="bias_bc")
+        bias_row = keep.tile([P, D], BF16, name="bias_row")
+        nc.vector.memset(bias_row[:], 0.0)
+        ones = keep.tile([P, P], BF16, name="ones")
+        nc.vector.memset(ones[:], 1.0)
 
         def load_v(q):
             nc.sync.dma_start(
@@ -89,9 +91,12 @@ def tile_hybridsuperlayer_pb_kernel(tc, h_gelu, c_proj_U, c_proj_S, c_proj_V, c_
                 load_split(h_sb[(k, 1)][:, 1024 * c : 1024 * (c + 1)], h_flat[256:512, :], 512 * (2 * k + c))
 
         load_u_half(0)
+        with nc.allow_non_contiguous_dma(reason="512 singular values, two pairs to a partition"):
+            nc.sync.dma_start(out=s4[:], in_=c_proj_S.rearrange("(u p e) -> p u e", u=2, p=P, e=2))
         load_v(0)
         load_u_half(1)
         load_v(1)
+        nc.sync.dma_start(out=bias_row[0:1, :], in_=c_proj_bias.unsqueeze(0))
         load_u(1)
         load_h(0, 0)
         load_u(2)
@@ -106,7 +111,6 @@ def tile_hybridsuperlayer_pb_kernel(tc, h_gelu, c_proj_U, c_proj_S, c_proj_V, c_
         load_v(3)
         load_u(7)
         load_h(0, 1)
-        nc.sync.dma_start(out=bias_bc[:], in_=c_proj_bias.partition_broadcast(P))
         load_blocks(1)
         load_blocks(2)
         load_blocks(3)
@@ -131,11 +135,11 @@ def tile_hybridsuperlayer_pb_kernel(tc, h_gelu, c_proj_U, c_proj_S, c_proj_V, c_
                 h_q[(k, z)] = codes_and_scales("h%d_%d" % (k, z))
         v_q = [codes_and_scales("v%d" % hf) for hf in range(2)]
 
-        bank_names = ["w0", "w1", "w2", "w3", "acc3", "acc2", "acc1", "acc0"]
-        count = [0, 8]
+        bank_names = [["acc1", "acc0", "w0", "w1", "w2", "w3", "acc3", "acc2"]]
+        count = [0]
 
         def next_bank():
-            name = bank_names[count[0] % count[1]]
+            name = bank_names[0][count[0] % len(bank_names[0])]
             count[0] = count[0] + 1
             return psum.tile([P, 512], F32, name=name, tag=name)
 
@@ -277,6 +281,10 @@ def tile_hybridsuperlayer_pb_kernel(tc, h_gelu, c_proj_U, c_proj_S, c_proj_V, c_
         quantise(vg, v_q[0], 0, 256)
         quantise(ug0, us_q[0], 256, 512)
         quantise(vg, v_q[0], 256, 512)
+        for hf in range(2):
+            bank = next_bank()
+            nc.tensor.matmul(bank[:], lhsT=ones[:], rhs=bias_row[:, 512 * hf : 512 * (hf + 1)], start=True, stop=True)
+            nc.scalar.copy(out=bias_bc[:, 512 * hf : 512 * (hf + 1)], in_=bank[:])
         ug1 = prepare_u(1)
         quantise(ug1, us_q[1])
 
@@ -311,10 +319,10 @@ def tile_hybridsuperlayer_pb_kernel(tc, h_gelu, c_proj_U, c_proj_S, c_proj_V, c_
 
         for r, (g, hf) in enumerate(order):
             if r == 2:
-                count[1] = 6
-                count[0] = 4
+                bank_names[0] = ["acc3", "acc2", "w0", "w1", "w2", "w3"]
+                count[0] = 0
             if r == 7:
-                count[1] = 4
+                bank_names[0] = ["w0", "w1", "w2", "w3"]
                 count[0] = 0
             on_v = COPY_V.get(r, () if hf == 0 else COPY_V_LATE)
             for b in range(4):

@@ -16,9 +16,9 @@ TOK, D, DFF, R = 512, 1024, 4096, 512
 G = DFF // 512
 FLOPS = 2 * DFF * D * R + 2 * TOK * DFF * D
 
-H_ROUND = {0: [(0, 0)], 2: [(1, 0)], 4: [(2, 0)], 5: [(3, 0), (0, 1)], 8: [(1, 1)], 10: [(2, 1)], 12: [(3, 1)]}
+H_ROUND = {0: [(0, 0)], 2: [(1, 0)], 4: [(2, 0)], 5: [(3, 0)], 6: [(0, 1)], 8: [(1, 1)], 10: [(2, 1)], 12: [(3, 1)]}
 BLOCKS = (1, 2, 3)
-V2_ROUND = 5
+V2_ROUND = 6
 COPY_V = {3: (3,), 4: (3,), 7: (3,), 8: (), 9: (), 10: (), 12: (), 15: (1, 3)}
 COPY_V_LATE = (1,)
 TAKE_EARLY = (0, 1, 0, 1)
@@ -49,9 +49,9 @@ def tile_hybridsuperlayer_pb_kernel(tc, h_gelu, c_proj_U, c_proj_S, c_proj_V, c_
                 h_sb[(k, z)] = keep.tile([P, 2048], BF16, name="h_sb%d_%d" % (k, z), align_bytes=64)
         bias_bc = keep.tile([P, D], BF16, name="bias_bc")
         bias_row = keep.tile([P, D], BF16, name="bias_row")
-        nc.vector.memset(bias_row[:], 0.0)
-        ones = keep.tile([P, P], BF16, name="ones")
+        ones = keep.tile([P, 512], BF16, name="ones")
         nc.vector.memset(ones[:], 1.0)
+        nc.vector.memset(bias_row[:], 0.0)
 
         def load_v(q):
             nc.sync.dma_start(
@@ -267,6 +267,15 @@ def tile_hybridsuperlayer_pb_kernel(tc, h_gelu, c_proj_U, c_proj_S, c_proj_V, c_
             if g == G - 1:
                 finish(hf, m, lo, hi)
 
+        def keep_busy(n, width=512):
+            for k in range(n):
+                nc.tensor.matmul(busy_bank[0][:, 0:width], lhsT=ones[:, 0:P], rhs=ones[:, 0:width], start=True, stop=True)
+
+        busy_bank = [None]
+
+        busy_bank[0] = next_bank()
+        keep_busy(8)
+        count[0] = 0
         ug0 = grouped_tile("usg")
         vg = grouped_tile("vg")
         bank_u = transpose_half(u_sb[0][:])
@@ -283,7 +292,7 @@ def tile_hybridsuperlayer_pb_kernel(tc, h_gelu, c_proj_U, c_proj_S, c_proj_V, c_
         quantise(vg, v_q[0], 256, 512)
         for hf in range(2):
             bank = next_bank()
-            nc.tensor.matmul(bank[:], lhsT=ones[:], rhs=bias_row[:, 512 * hf : 512 * (hf + 1)], start=True, stop=True)
+            nc.tensor.matmul(bank[:], lhsT=ones[:, 0:P], rhs=bias_row[:, 512 * hf : 512 * (hf + 1)], start=True, stop=True)
             nc.scalar.copy(out=bias_bc[:, 512 * hf : 512 * (hf + 1)], in_=bank[:])
         ug1 = prepare_u(1)
         quantise(ug1, us_q[1])
@@ -330,6 +339,8 @@ def tile_hybridsuperlayer_pb_kernel(tc, h_gelu, c_proj_U, c_proj_S, c_proj_V, c_
                 if hf == 1 and b == 0 and g > 0:
                     quantise_w(g - 1, 1)
                 take((TAKE_EARLY if hf == 0 else TAKE_LATE)[b], r)
+                if r == V2_ROUND and b == 2:
+                    vg = prepare_v2()
             late = []
             units = H_ROUND.get(r, ())
             for k, z in units:
@@ -342,10 +353,10 @@ def tile_hybridsuperlayer_pb_kernel(tc, h_gelu, c_proj_U, c_proj_S, c_proj_V, c_
             for k, z in units:
                 if z == 0 or k not in BLOCKS:
                     late.append((prepare_h(k, z), h_q[(k, z)]))
-            if r == V2_ROUND:
-                late.append((prepare_v2(), v_q[1]))
             if r + 2 < G:
                 quantise(ug, us_q[r + 2])
+            if r == V2_ROUND:
+                quantise(vg, v_q[1])
             for grouped, codes in late:
                 quantise(grouped, codes)
         quantise_w(G - 1, 1)

@@ -19,9 +19,9 @@ FLOPS = 2 * DFF * D * R + 2 * TOK * DFF * D
 H_ROUND = {0: [(0, 0)], 2: [(1, 0)], 4: [(2, 0)], 5: [(3, 0)], 6: [(0, 1)], 8: [(1, 1)], 10: [(2, 1)], 12: [(3, 1)]}
 BLOCKS = (1, 2, 3)
 V2_ROUND = 6
-COPY_V = {3: (3,), 4: (3,), 7: (3,), 8: (), 9: (), 10: (), 12: (), 15: (1, 3)}
-COPY_V_LATE = (1,)
-TAKE_EARLY = (0, 1, 0, 1)
+COPY_V = {1: (3,), 3: (3,), 5: (3,), 7: (3,), 11: (3,), 13: (3,), 15: (0, 2)}
+COPY_V_LATE = ()
+TAKE_EARLY = (1, 0, 0, 1)
 TAKE_LATE = (1, 1, 1, 1)
 
 
@@ -124,8 +124,8 @@ def tile_hybridsuperlayer_pb_kernel(tc, h_gelu, c_proj_U, c_proj_S, c_proj_V, c_
             return halves(u_sb[g + 1])
 
         def codes_and_scales(name):
-            codes = keep.tile([P, 512], U32, name=name + "_c", align_bytes=64)
-            scales = keep.tile([P, 512], U8, name=name + "_s", align_bytes=64)
+            codes = keep.tile([P, 512], U32, name=name + "_c", align_bytes=256)
+            scales = keep.tile([P, 512], U8, name=name + "_s", align_bytes=256)
             return codes, scales
 
         us_q = [codes_and_scales("us%d" % g) for g in range(G)]
@@ -274,7 +274,7 @@ def tile_hybridsuperlayer_pb_kernel(tc, h_gelu, c_proj_U, c_proj_S, c_proj_V, c_
         busy_bank = [None]
 
         busy_bank[0] = next_bank()
-        keep_busy(8)
+        keep_busy(4)
         count[0] = 0
         ug0 = grouped_tile("usg")
         vg = grouped_tile("vg")
@@ -339,7 +339,7 @@ def tile_hybridsuperlayer_pb_kernel(tc, h_gelu, c_proj_U, c_proj_S, c_proj_V, c_
                 if hf == 1 and b == 0 and g > 0:
                     quantise_w(g - 1, 1)
                 take((TAKE_EARLY if hf == 0 else TAKE_LATE)[b], r)
-                if r == V2_ROUND and b == 2:
+                if r == V2_ROUND and b == 3:
                     vg = prepare_v2()
             late = []
             units = H_ROUND.get(r, ())

@@ -19,7 +19,7 @@ FLOPS = 2 * DFF * D * R + 2 * TOK * DFF * D
 H_ROUND = {0: [(0, 0)], 2: [(1, 0)], 4: [(2, 0)], 5: [(3, 0)], 6: [(0, 1)], 8: [(1, 1)], 10: [(2, 1)], 12: [(3, 1)]}
 BLOCKS = (1, 2, 3)
 V2_ROUND = 6
-COPY_V = {1: (3,), 3: (3,), 5: (3,), 7: (3,), 11: (3,), 13: (3,), 15: (0, 2)}
+COPY_V = {1: (3,), 3: (3,), 7: (3,), 11: (3,), 13: (3,), 14: (3,), 15: (0, 2)}
 COPY_V_LATE = ()
 TAKE_EARLY = (1, 0, 0, 1)
 TAKE_LATE = (1, 1, 1, 1)
@@ -93,13 +93,14 @@ def tile_hybridsuperlayer_pb_kernel(tc, h_gelu, c_proj_U, c_proj_S, c_proj_V, c_
         load_u_half(0)
         with nc.allow_non_contiguous_dma(reason="512 singular values, two pairs to a partition"):
             nc.sync.dma_start(out=s4[:], in_=c_proj_S.rearrange("(u p e) -> p u e", u=2, p=P, e=2))
-        load_v(0)
         load_u_half(1)
+        for t in range(2):
+            nc.sync.dma_start(out=v_sb[0][:, 512 * t : 512 * (t + 1)], in_=c_proj_V[128 * t : 128 * (t + 1), :])
         load_v(1)
         nc.sync.dma_start(out=bias_row[0:1, :], in_=c_proj_bias.unsqueeze(0))
         load_u(1)
-        load_h(0, 0)
         load_u(2)
+        load_h(0, 0)
         load_h(1, 0)
         load_u(3)
         load_u(4)
@@ -124,8 +125,8 @@ def tile_hybridsuperlayer_pb_kernel(tc, h_gelu, c_proj_U, c_proj_S, c_proj_V, c_
             return halves(u_sb[g + 1])
 
         def codes_and_scales(name):
-            codes = keep.tile([P, 512], U32, name=name + "_c", align_bytes=256)
-            scales = keep.tile([P, 512], U8, name=name + "_s", align_bytes=256)
+            codes = keep.tile([P, 512], U32, name=name + "_c", align_bytes=64)
+            scales = keep.tile([P, 512], U8, name=name + "_s", align_bytes=64)
             return codes, scales
 
         us_q = [codes_and_scales("us%d" % g) for g in range(G)]
@@ -274,21 +275,29 @@ def tile_hybridsuperlayer_pb_kernel(tc, h_gelu, c_proj_U, c_proj_S, c_proj_V, c_
         busy_bank = [None]
 
         busy_bank[0] = next_bank()
-        keep_busy(4)
+        keep_busy(3)
         count[0] = 0
         ug0 = grouped_tile("usg")
         vg = grouped_tile("vg")
-        bank_u = transpose_half(u_sb[0][:])
-        scale_bank(bank_u, ug0[:, 0:1024])
-        bank_v = transpose_half(v_sb[0][:])
-        copy_bank_words(bank_v, vg[:, 0:1024])
-        quantise(ug0, us_q[0], 0, 256)
-        bank_u = transpose_half(u_sb[1][:])
-        scale_bank(bank_u, ug0[:, 1024:2048])
+        for half in range(2):
+            bank_u = transpose_half(u_sb[half][:])
+            scale_bank(bank_u, ug0[:, 1024 * half : 1024 * (half + 1)])
+        for t in range(2):
+            bank_v = next_bank() if t == 1 else psum.tile([P, 512], F32, name="acc2", tag="acc2")
+            for u in range(2):
+                nc.tensor.transpose(
+                    bank_v[:, 128 * u : 128 * u + 128],
+                    v_sb[0][:].bitcast(F32)[:, 256 * t + 128 * u : 256 * t + 128 * u + 128],
+                    ident[:],
+                )
+            nc.scalar.copy(
+                out=vg[:, 512 * t : 512 * (t + 1)].bitcast(F32).rearrange("p (c u) -> p c u", u=2),
+                in_=bank_v[:, 0:256].rearrange("p (u c) -> p c u", u=2),
+            )
+            quantise(ug0, us_q[0], 256 * t, 256 * (t + 1))
+            quantise(vg, v_q[0], 128 * t, 128 * (t + 1))
         bank_v = transpose_half(v_sb[1][:])
         copy_bank_words(bank_v, vg[:, 1024:2048])
-        quantise(vg, v_q[0], 0, 256)
-        quantise(ug0, us_q[0], 256, 512)
         quantise(vg, v_q[0], 256, 512)
         for hf in range(2):
             bank = next_bank()
@@ -317,8 +326,8 @@ def tile_hybridsuperlayer_pb_kernel(tc, h_gelu, c_proj_U, c_proj_S, c_proj_V, c_
         for k in range(2, G):
             passes += first[2 * k : 2 * k + 2] + second[2 * k - 4 : 2 * k - 2]
         passes += second[12:14] + [(g, 1, 2) for g in range(G - 1)] + second[14:16] + [(G - 1, 1, 2)]
-        passes += [(g, 1, 3, 0, 256) for g in range(G)] + [(g, 1, 3, 256, 512) for g in range(G)]
-        assert len(passes) == 72
+        passes += [(g, 1, 3, 0, 256) for g in range(G)] + [(g, 1, 3, 256, 384) for g in range(G)] + [(g, 1, 3, 384, 512) for g in range(G)]
+        assert len(passes) == 80
 
         def take(n, r):
             while n > 0 and passes and is_ready(passes[0], r):

@@ -48,8 +48,10 @@ def tile_hybridsuperlayer_pb_kernel(tc, h_gelu, c_proj_U, c_proj_S, c_proj_V, c_
             for z in range(2):
                 h_sb[(k, z)] = keep.tile([P, 2048], BF16, name="h_sb%d_%d" % (k, z), align_bytes=64)
         bias_bc = keep.tile([P, D], BF16, name="bias_bc")
+        s_row = keep.tile([P, R], BF16, name="s_row")
         bias_row = keep.tile([P, D], BF16, name="bias_row")
         ones = keep.tile([P, 512], BF16, name="ones")
+        nc.vector.memset(s_row[:], 0.0)
         nc.vector.memset(ones[:], 1.0)
         nc.vector.memset(bias_row[:], 0.0)
 
@@ -91,14 +93,17 @@ def tile_hybridsuperlayer_pb_kernel(tc, h_gelu, c_proj_U, c_proj_S, c_proj_V, c_
                 load_split(h_sb[(k, 1)][:, 1024 * c : 1024 * (c + 1)], h_flat[256:512, :], 512 * (2 * k + c))
 
         load_u_half(0)
-        with nc.allow_non_contiguous_dma(reason="512 singular values, two pairs to a partition"):
-            nc.sync.dma_start(out=s4[:], in_=c_proj_S.rearrange("(u p e) -> p u e", u=2, p=P, e=2))
+        nc.sync.dma_start(out=s_row[0:1, :], in_=c_proj_S.unsqueeze(0))
         load_u_half(1)
+        nc.sync.dma_start(out=bias_row[0:1, :], in_=c_proj_bias.unsqueeze(0))
         for t in range(2):
             nc.sync.dma_start(out=v_sb[0][:, 512 * t : 512 * (t + 1)], in_=c_proj_V[128 * t : 128 * (t + 1), :])
         load_v(1)
-        nc.sync.dma_start(out=bias_row[0:1, :], in_=c_proj_bias.unsqueeze(0))
-        load_u(1)
+        for half in range(2):
+            nc.sync.dma_start(
+                out=u_sb[2][:, 1024 * half : 1024 * (half + 1)],
+                in_=c_proj_U[512 + 256 * half : 512 + 256 * (half + 1), :].rearrange("(p e) r -> p (e r)", p=P, e=2),
+            )
         load_u(2)
         load_h(0, 0)
         load_h(1, 0)
@@ -136,13 +141,20 @@ def tile_hybridsuperlayer_pb_kernel(tc, h_gelu, c_proj_U, c_proj_S, c_proj_V, c_
                 h_q[(k, z)] = codes_and_scales("h%d_%d" % (k, z))
         v_q = [codes_and_scales("v%d" % hf) for hf in range(2)]
 
-        bank_names = [["acc1", "acc0", "w0", "w1", "w2", "w3", "acc3", "acc2"]]
-        count = [0]
+        bank_order = ["bank%d" % b for b in range(8)]
 
         def next_bank():
-            name = bank_names[0][count[0] % len(bank_names[0])]
-            count[0] = count[0] + 1
+            name = bank_order[0]
+            bank_order.remove(name)
+            bank_order.append(name)
             return psum.tile([P, 512], F32, name=name, tag=name)
+
+        held = {}
+
+        def hold_bank(key):
+            held[key] = bank_order[0]
+            bank_order.remove(held[key])
+            return psum.tile([P, 512], F32, name=held[key], tag=held[key])
 
         def quantise(grouped, pair, lo=0, hi=512):
             nc.vector.quantize_mx(
@@ -245,13 +257,15 @@ def tile_hybridsuperlayer_pb_kernel(tc, h_gelu, c_proj_U, c_proj_S, c_proj_V, c_
             nc.vector.tensor_tensor(
                 out=res[:, lo:hi], in0=acc[(hf, m, lo)][:, lo:hi], in1=bias_bc[:, 512 * hf + lo : 512 * hf + hi], op=ADD
             )
+            if lo == 0:
+                bank_order.append(held[(hf, m)])
             nc.sync.dma_start(
                 out=out_flat[128 * m : 128 * (m + 1), 512 * hf + lo : 512 * hf + hi], in_=res[:, lo:hi]
             )
 
         def stage2_pass(g, hf, m, lo=0, hi=512):
             if g == 0 and lo == 0:
-                acc[(hf, m, lo)] = psum.tile([P, 512], F32, name="acc%d" % m, tag="acc%d" % m)
+                acc[(hf, m, lo)] = hold_bank((hf, m))
             elif g == 0:
                 acc[(hf, m, lo)] = next_bank()
             codes, scales = h_q[(g // 2, m // 2)]
@@ -276,14 +290,35 @@ def tile_hybridsuperlayer_pb_kernel(tc, h_gelu, c_proj_U, c_proj_S, c_proj_V, c_
 
         busy_bank[0] = next_bank()
         keep_busy(3)
-        count[0] = 0
+
+        def spread_s():
+            bank = next_bank()
+            for k in range(4):
+                first_r = 256 * (k // 2) + k % 2
+                nc.tensor.matmul(
+                    bank[:, k : k + 1], lhsT=s_row[:, first_r : first_r + 255 : 2], rhs=ones[:, 0:1], start=True, stop=True
+                )
+            nc.scalar.copy(out=s4[:].rearrange("p u e -> p (u e)"), in_=bank[:, 0:4])
+
+        def spread_bias(hf):
+            bank = next_bank()
+            nc.tensor.matmul(bank[:], lhsT=ones[:, 0:P], rhs=bias_row[:, 512 * hf : 512 * (hf + 1)], start=True, stop=True)
+            return bank
+
+        def copy_bias(hf, bank):
+            nc.scalar.copy(out=bias_bc[:, 512 * hf : 512 * (hf + 1)], in_=bank[:])
+
+        bias_bank = []
         ug0 = grouped_tile("usg")
         vg = grouped_tile("vg")
         for half in range(2):
             bank_u = transpose_half(u_sb[half][:])
+            if half == 0:
+                spread_s()
             scale_bank(bank_u, ug0[:, 1024 * half : 1024 * (half + 1)])
+        bias_bank.append(spread_bias(0))
         for t in range(2):
-            bank_v = next_bank() if t == 1 else psum.tile([P, 512], F32, name="acc2", tag="acc2")
+            bank_v = next_bank()
             for u in range(2):
                 nc.tensor.transpose(
                     bank_v[:, 128 * u : 128 * u + 128],
@@ -296,15 +331,12 @@ def tile_hybridsuperlayer_pb_kernel(tc, h_gelu, c_proj_U, c_proj_S, c_proj_V, c_
             )
             quantise(ug0, us_q[0], 256 * t, 256 * (t + 1))
             quantise(vg, v_q[0], 128 * t, 128 * (t + 1))
+        bias_bank.append(spread_bias(1))
+        copy_bias(0, bias_bank[0])
         bank_v = transpose_half(v_sb[1][:])
         copy_bank_words(bank_v, vg[:, 1024:2048])
+        copy_bias(1, bias_bank[1])
         quantise(vg, v_q[0], 256, 512)
-        for hf in range(2):
-            bank = next_bank()
-            nc.tensor.matmul(bank[:], lhsT=ones[:, 0:P], rhs=bias_row[:, 512 * hf : 512 * (hf + 1)], start=True, stop=True)
-            nc.scalar.copy(out=bias_bc[:, 512 * hf : 512 * (hf + 1)], in_=bank[:])
-        ug1 = prepare_u(1)
-        quantise(ug1, us_q[1])
 
         order = [(g, 0) for g in range(G)] + [(g, 1) for g in range(G)]
         slot = {}
@@ -336,18 +368,15 @@ def tile_hybridsuperlayer_pb_kernel(tc, h_gelu, c_proj_U, c_proj_S, c_proj_V, c_
                 n = n - 1
 
         for r, (g, hf) in enumerate(order):
-            if r == 2:
-                bank_names[0] = ["acc3", "acc2", "w0", "w1", "w2", "w3"]
-                count[0] = 0
-            if r == 7:
-                bank_names[0] = ["w0", "w1", "w2", "w3"]
-                count[0] = 0
             on_v = COPY_V.get(r, () if hf == 0 else COPY_V_LATE)
             for b in range(4):
                 stage1_bank(g, hf, b, b in on_v)
                 if hf == 1 and b == 0 and g > 0:
                     quantise_w(g - 1, 1)
                 take((TAKE_EARLY if hf == 0 else TAKE_LATE)[b], r)
+                if r == 0 and b == 1:
+                    ug = prepare_u(1)
+                    quantise(ug, us_q[1])
                 if r == V2_ROUND and b == 3:
                     vg = prepare_v2()
             late = []

@@ -19,8 +19,12 @@ FLOPS = 2 * DFF * D * R + 2 * TOK * DFF * D
 H_ROUND = {0: [(0, 0)], 2: [(1, 0)], 4: [(2, 0)], 5: [(3, 0)], 6: [(0, 1)], 8: [(1, 1)], 10: [(2, 1)], 12: [(3, 1)]}
 BLOCKS = (1, 2, 3)
 V2_ROUND = 6
-COPY_V = {1: (3,), 3: (3,), 7: (3,), 11: (3,), 13: (3,), 14: (3,), 15: (0, 2)}
+COPY_V = {1: (3,), 3: (3,), 7: (3,), 11: (3,), 13: (3,), 14: (3,)}
 COPY_V_LATE = ()
+WARM = 4
+DUM = (0, 1, 0, 0, 1, 0, 0)
+B0 = 4
+B1 = 6
 TAKE_EARLY = (1, 0, 0, 1)
 TAKE_LATE = (1, 1, 1, 1)
 
@@ -288,8 +292,10 @@ def tile_hybridsuperlayer_pb_kernel(tc, h_gelu, c_proj_U, c_proj_S, c_proj_V, c_
 
         busy_bank = [None]
 
-        busy_bank[0] = next_bank()
-        keep_busy(3)
+        held["busy"] = bank_order[0]
+        busy_bank[0] = psum.tile([P, 512], F32, name=bank_order[0], tag=bank_order[0])
+        bank_order.remove(held["busy"])
+        keep_busy(WARM)
 
         def spread_s():
             bank = next_bank()
@@ -303,40 +309,54 @@ def tile_hybridsuperlayer_pb_kernel(tc, h_gelu, c_proj_U, c_proj_S, c_proj_V, c_
         def spread_bias(hf):
             bank = next_bank()
             nc.tensor.matmul(bank[:], lhsT=ones[:, 0:P], rhs=bias_row[:, 512 * hf : 512 * (hf + 1)], start=True, stop=True)
-            return bank
-
-        def copy_bias(hf, bank):
             nc.scalar.copy(out=bias_bc[:, 512 * hf : 512 * (hf + 1)], in_=bank[:])
 
-        bias_bank = []
-        ug0 = grouped_tile("usg")
-        vg = grouped_tile("vg")
-        for half in range(2):
-            bank_u = transpose_half(u_sb[half][:])
-            if half == 0:
-                spread_s()
-            scale_bank(bank_u, ug0[:, 1024 * half : 1024 * (half + 1)])
-        bias_bank.append(spread_bias(0))
-        for t in range(2):
-            bank_v = next_bank()
+        def transpose_v_rows(t):
+            bank = next_bank()
             for u in range(2):
                 nc.tensor.transpose(
-                    bank_v[:, 128 * u : 128 * u + 128],
+                    bank[:, 128 * u : 128 * u + 128],
                     v_sb[0][:].bitcast(F32)[:, 256 * t + 128 * u : 256 * t + 128 * u + 128],
                     ident[:],
                 )
             nc.scalar.copy(
                 out=vg[:, 512 * t : 512 * (t + 1)].bitcast(F32).rearrange("p (c u) -> p c u", u=2),
-                in_=bank_v[:, 0:256].rearrange("p (u c) -> p c u", u=2),
+                in_=bank[:, 0:256].rearrange("p (u c) -> p c u", u=2),
             )
+
+        ug0 = grouped_tile("usg")
+        ug1 = grouped_tile("usg")
+        vg = grouped_tile("vg")
+        def point(i):
+            keep_busy(DUM[i])
+            if i == B0:
+                spread_bias(0)
+            if i == B1:
+                spread_bias(1)
+
+        spread_s()
+        point(0)
+        for half in range(2):
+            bank_u = transpose_half(u_sb[half][:])
+            scale_bank(bank_u, ug0[:, 1024 * half : 1024 * (half + 1)])
+            point(1 + half)
+        for t in range(2):
+            transpose_v_rows(t)
+            point(3 + t)
             quantise(ug0, us_q[0], 256 * t, 256 * (t + 1))
             quantise(vg, v_q[0], 128 * t, 128 * (t + 1))
-        bias_bank.append(spread_bias(1))
-        copy_bias(0, bias_bank[0])
         bank_v = transpose_half(v_sb[1][:])
         copy_bank_words(bank_v, vg[:, 1024:2048])
-        copy_bias(1, bias_bank[1])
+        point(5)
+        bank_u = transpose_half(u_halves(1)[0])
+        scale_bank(bank_u, ug1[:, 0:1024])
         quantise(vg, v_q[0], 256, 512)
+        point(6)
+        bank_u = transpose_half(u_halves(1)[1])
+        scale_bank(bank_u, ug1[:, 1024:2048])
+        bank_order.append(held["busy"])
+        for t in range(2):
+            quantise(ug1, us_q[1], 256 * t, 256 * (t + 1))
 
         order = [(g, 0) for g in range(G)] + [(g, 1) for g in range(G)]
         slot = {}
@@ -374,9 +394,6 @@ def tile_hybridsuperlayer_pb_kernel(tc, h_gelu, c_proj_U, c_proj_S, c_proj_V, c_
                 if hf == 1 and b == 0 and g > 0:
                     quantise_w(g - 1, 1)
                 take((TAKE_EARLY if hf == 0 else TAKE_LATE)[b], r)
-                if r == 0 and b == 1:
-                    ug = prepare_u(1)
-                    quantise(ug, us_q[1])
                 if r == V2_ROUND and b == 3:
                     vg = prepare_v2()
             late = []

@@ -54,9 +54,9 @@ def tile_hybridsuperlayer_pb_kernel(tc, h_gelu, c_proj_U, c_proj_S, c_proj_V, c_
         bias_bc = keep.tile([P, D], BF16, name="bias_bc")
         s_row = keep.tile([P, R], BF16, name="s_row")
         bias_row = keep.tile([P, D], BF16, name="bias_row")
-        ones = keep.tile([P, 512], BF16, name="ones")
-        nc.vector.memset(s_row[:], 0.0)
+        ones = keep.tile([P, P], BF16, name="ones")
         nc.vector.memset(ones[:], 1.0)
+        nc.vector.memset(s_row[:], 0.0)
         nc.vector.memset(bias_row[:], 0.0)
 
         def load_v(q):
@@ -286,9 +286,15 @@ def tile_hybridsuperlayer_pb_kernel(tc, h_gelu, c_proj_U, c_proj_S, c_proj_V, c_
             if g == G - 1:
                 finish(hf, m, lo, hi)
 
-        def keep_busy(n, width=512):
+        def keep_busy(n):
             for k in range(n):
-                nc.tensor.matmul(busy_bank[0][:, 0:width], lhsT=ones[:, 0:P], rhs=ones[:, 0:width], start=True, stop=True)
+                nc.tensor.matmul(
+                    busy_bank[0][:].rearrange("p (n c) -> p n c", n=4),
+                    lhsT=ones[:],
+                    rhs=ones[:].unsqueeze(1).to_broadcast([P, 4, P]),
+                    start=True,
+                    stop=True,
+                )
 
         busy_bank = [None]
 

@@ -19,7 +19,7 @@ FLOPS = 2 * DFF * D * R + 2 * TOK * DFF * D
 H_ROUND = {0: [(0, 0)], 2: [(1, 0)], 4: [(2, 0)], 5: [(3, 0)], 6: [(0, 1)], 8: [(1, 1)], 10: [(2, 1)], 12: [(3, 1)]}
 BLOCKS = (1, 2, 3)
 V2_ROUND = 6
-COPY_V = {1: (3,), 3: (3,), 7: (3,), 11: (3,), 13: (3,), 14: (3,)}
+COPY_V = {11: (3,), 13: (3,), 14: (3,)}
 COPY_V_LATE = ()
 WARM = 4
 DUM = (0, 1, 0, 0, 1, 0, 0)

from contextlib import ExitStack

import concourse.mybir as mybir
from concourse.masks import make_identity

F32 = mybir.dt.float32
BF16 = mybir.dt.bfloat16
U32 = mybir.dt.uint32
U8 = mybir.dt.uint8
FP8X4 = mybir.dt.float8_e4m3fn_x4
MULT = mybir.AluOpType.mult
ADD = mybir.AluOpType.add

P = 128
TOK, D, DFF, R = 512, 1024, 4096, 512
G = DFF // 512
FLOPS = 2 * DFF * D * R + 2 * TOK * DFF * D

H_ROUND = {0: [(0, 0)], 2: [(1, 0)], 4: [(2, 0)], 5: [(3, 0)], 6: [(0, 1)], 8: [(1, 1)], 10: [(2, 1)], 12: [(3, 1)]}
BLOCKS = (1, 2, 3)
V2_ROUND = 6
COPY_V = {11: (3,), 13: (3,), 14: (3,)}
COPY_V_LATE = ()
WARM = 4
DUM = (0, 1, 0, 0, 1, 0, 0)
B0 = 4
B1 = 6
TAKE_EARLY = (1, 0, 0, 1)
TAKE_LATE = (1, 1, 1, 1)


def tile_hybridsuperlayer_pb_kernel(tc, h_gelu, c_proj_U, c_proj_S, c_proj_V, c_proj_bias, out):
    nc = tc.nc
    h_flat = h_gelu.flatten_outer_dims()
    out_flat = out.flatten_outer_dims()
    with ExitStack() as ctx:
        keep = ctx.enter_context(tc.tile_pool(name="keep", bufs=1))
        stage = ctx.enter_context(tc.tile_pool(name="stage", bufs=2))
        psum = ctx.enter_context(tc.psum_pool(name="psum", bufs=1))
        ctx.enter_context(tc.manual_schedule())

        ident = keep.tile([P, P], F32, name="ident")
        make_identity(nc, ident[:])

        s4 = keep.tile([P, 2, 2], BF16, name="s4")
        v_sb = [keep.tile([P, 1024], BF16, name="v_sb%d" % q) for q in range(4)]
        u_sb = [keep.tile([P, 1024], BF16, name="u_sb%d" % q) for q in range(2)] + [
            keep.tile([P, 2048], BF16, name="u_sb%d" % (g + 1)) for g in range(1, G)
        ]
        h_sb = {}
        for k in range(4):
            for z in range(2):
                h_sb[(k, z)] = keep.tile([P, 2048], BF16, name="h_sb%d_%d" % (k, z), align_bytes=64)
        bias_bc = keep.tile([P, D], BF16, name="bias_bc")
        s_row = keep.tile([P, R], BF16, name="s_row")
        bias_row = keep.tile([P, D], BF16, name="bias_row")
        ones = keep.tile([P, P], BF16, name="ones")
        nc.vector.memset(ones[:], 1.0)
        nc.vector.memset(s_row[:], 0.0)
        nc.vector.memset(bias_row[:], 0.0)

        def load_v(q):
            nc.sync.dma_start(
                out=v_sb[q][:].rearrange("p (t r) -> p t r", t=2),
                in_=c_proj_V[256 * q : 256 * (q + 1), :].rearrange("(t p) r -> p t r", p=P),
            )

        def load_u_half(q):
            nc.sync.dma_start(
                out=u_sb[q][:],
                in_=c_proj_U[256 * q : 256 * (q + 1), :].rearrange("(p e) r -> p (e r)", p=P, e=2),
            )

        def load_u(g):
            nc.sync.dma_start(
                out=u_sb[g + 1][:].rearrange("p (u x) -> p u x", u=2),
                in_=c_proj_U[512 * g : 512 * (g + 1), :].rearrange("(u p e) r -> p u (e r)", u=2, p=P, e=2),
            )

        def load_h(k, z):
            nc.sync.dma_start(
                out=h_sb[(k, z)][:].rearrange("p (m k) -> p m k", m=2),
                in_=h_flat[256 * z : 256 * (z + 1), 1024 * k : 1024 * (k + 1)].rearrange("(m p) k -> p m k", p=P),
            )

        def load_split(dst, rows, col0):
            for q in range(4):
                for u in range(2):
                    col = col0 + 256 * u + 64 * q
                    nc.sync.dma_start(
                        out=dst[32 * q + u : 32 * q + 32 : 2, :].rearrange("r (c w) -> r c w", w=64),
                        in_=rows[:, col : col + 64].rearrange("(c r) w -> r c w", r=16),
                    )

        def load_blocks(k):
            for c in range(2):
                load_split(h_sb[(k, 1)][:, 1024 * c : 1024 * (c + 1)], h_flat[256:512, :], 512 * (2 * k + c))

        load_u_half(0)
        nc.sync.dma_start(out=s_row[0:1, :], in_=c_proj_S.unsqueeze(0))
        load_u_half(1)
        nc.sync.dma_start(out=bias_row[0:1, :], in_=c_proj_bias.unsqueeze(0))
        for t in range(2):
            nc.sync.dma_start(out=v_sb[0][:, 512 * t : 512 * (t + 1)], in_=c_proj_V[128 * t : 128 * (t + 1), :])
        load_v(1)
        for half in range(2):
            nc.sync.dma_start(
                out=u_sb[2][:, 1024 * half : 1024 * (half + 1)],
                in_=c_proj_U[512 + 256 * half : 512 + 256 * (half + 1), :].rearrange("(p e) r -> p (e r)", p=P, e=2),
            )
        load_u(2)
        load_h(0, 0)
        load_h(1, 0)
        load_u(3)
        load_u(4)
        load_h(2, 0)
        load_u(5)
        load_h(3, 0)
        load_u(6)
        load_v(2)
        load_v(3)
        load_u(7)
        load_h(0, 1)
        load_blocks(1)
        load_blocks(2)
        load_blocks(3)

        def halves(tile_ap):
            return [tile_ap[:, 0:1024], tile_ap[:, 1024:2048]]

        def u_halves(g):
            if g == 0:
                return [u_sb[0][:], u_sb[1][:]]
            return halves(u_sb[g + 1])

        def codes_and_scales(name):
            codes = keep.tile([P, 512], U32, name=name + "_c", align_bytes=64)
            scales = keep.tile([P, 512], U8, name=name + "_s", align_bytes=64)
            return codes, scales

        us_q = [codes_and_scales("us%d" % g) for g in range(G)]
        h_q = {}
        for k in range(4):
            for z in range(2):
                h_q[(k, z)] = codes_and_scales("h%d_%d" % (k, z))
        v_q = [codes_and_scales("v%d" % hf) for hf in range(2)]

        bank_order = ["bank%d" % b for b in range(8)]

        def next_bank():
            name = bank_order[0]
            bank_order.remove(name)
            bank_order.append(name)
            return psum.tile([P, 512], F32, name=name, tag=name)

        held = {}

        def hold_bank(key):
            held[key] = bank_order[0]
            bank_order.remove(held[key])
            return psum.tile([P, 512], F32, name=held[key], tag=held[key])

        def quantise(grouped, pair, lo=0, hi=512):
            nc.vector.quantize_mx(
                out=pair[0][:, lo:hi].bitcast(FP8X4), scales=pair[1][:, lo:hi], in_=grouped[:, 4 * lo : 4 * hi]
            )

        def transpose_rows(words, pitch):
            bank = next_bank()
            for j in range(2):
                for u in range(2):
                    nc.tensor.transpose(
                        bank[:, 256 * u + 128 * j : 256 * u + 128 * j + 128],
                        words[:, pitch * j + 128 * u : pitch * j + 128 * u + 128],
                        ident[:],
                    )
            return bank

        def transpose_half(src):
            return transpose_rows(src.bitcast(F32), 256)

        def copy_bank_words(bank, dst_bf16, on_vector=False):
            dst = dst_bf16.bitcast(F32).rearrange("p (c u) -> p c u", u=2)
            src = bank[:].rearrange("p (u c) -> p c u", u=2)
            if on_vector:
                nc.vector.tensor_copy(out=dst, in_=src)
            else:
                nc.scalar.copy(out=dst, in_=src)

        s4_all = s4[:].unsqueeze(1).to_broadcast([P, 256, 2, 2])

        def scale_bank(bank, dst_bf16):
            nc.vector.tensor_tensor(
                out=dst_bf16.rearrange("p (c u e) -> p c u e", u=2, e=2),
                in0=bank[:].bitcast(BF16).rearrange("p (u c e) -> p c u e", u=2, e=2),
                in1=s4_all,
                op=MULT,
            )

        def grouped_tile(tag):
            return stage.tile([P, 2048], BF16, name=tag, tag=tag, align_bytes=64)

        def prepare_u(g):
            grouped = grouped_tile("usg")
            banks = [transpose_half(src) for src in u_halves(g)]
            for half in range(2):
                scale_bank(banks[half], grouped[:, 1024 * half : 1024 * (half + 1)])
            return grouped

        def prepare_h(k, z):
            grouped = grouped_tile("hg")
            words = h_sb[(k, z)][:].bitcast(F32)
            banks = [transpose_rows(words[:, 256 * c : 1024], 512) for c in range(2)]
            for c in range(2):
                copy_bank_words(banks[c], grouped[:, 1024 * c : 1024 * (c + 1)])
            return grouped

        def prepare_v2():
            grouped = grouped_tile("vg")
            banks = [transpose_half(v_sb[q][:]) for q in range(2, 4)]
            for half in range(2):
                copy_bank_words(banks[half], grouped[:, 1024 * half : 1024 * (half + 1)], True)
            return grouped

        def prepare_blocks(src, tag):
            grouped = grouped_tile(tag)
            nc.vector.transpose(out=grouped[:].bitcast(F32), in_=src[:].bitcast(F32))
            return grouped

        w_grouped = {}
        w_q = {}
        acc = {}

        def stage1_bank(g, hf, db, on_vector):
            if db == 0:
                w_grouped[(g, hf)] = stage.tile([P, 2048], BF16, name="wg", tag="wg", bufs=3, align_bytes=64)
            bank = next_bank()
            for t in range(4):
                nc.tensor.matmul_mx(
                    out=bank[:, 128 * t : 128 * (t + 1)],
                    lhsT=us_q[g][0][:, 128 * t : 128 * (t + 1)].bitcast(FP8X4),
                    lhsT_scale=us_q[g][1][:, 128 * t : 128 * (t + 1)],
                    rhs=v_q[hf][0][:, 128 * db : 128 * (db + 1)].bitcast(FP8X4),
                    rhs_scale=v_q[hf][1][:, 128 * db : 128 * (db + 1)],
                    start=True,
                    stop=True,
                )
            dst = w_grouped[(g, hf)][:, 512 * db : 512 * (db + 1)].rearrange("p (d t) -> p d t", t=4)
            src = bank[:].rearrange("p (t d) -> p d t", t=4)
            if on_vector:
                nc.vector.tensor_copy(out=dst, in_=src)
            else:
                nc.scalar.copy(out=dst, in_=src)

        def quantise_w(g, hf):
            w_q[(g, hf)] = codes_and_scales("w%d_%d" % (g, hf))
            quantise(w_grouped[(g, hf)], w_q[(g, hf)])

        def finish(hf, m, lo, hi):
            res = stage.tile([P, 512], F32, name="res", tag="res", bufs=6)
            nc.vector.tensor_tensor(
                out=res[:, lo:hi], in0=acc[(hf, m, lo)][:, lo:hi], in1=bias_bc[:, 512 * hf + lo : 512 * hf + hi], op=ADD
            )
            if lo == 0:
                bank_order.append(held[(hf, m)])
            nc.sync.dma_start(
                out=out_flat[128 * m : 128 * (m + 1), 512 * hf + lo : 512 * hf + hi], in_=res[:, lo:hi]
            )

        def stage2_pass(g, hf, m, lo=0, hi=512):
            if g == 0 and lo == 0:
                acc[(hf, m, lo)] = hold_bank((hf, m))
            elif g == 0:
                acc[(hf, m, lo)] = next_bank()
            codes, scales = h_q[(g // 2, m // 2)]
            col = 256 * (g % 2) + 128 * (m % 2)
            nc.tensor.matmul_mx(
                out=acc[(hf, m, lo)][:, lo:hi],
                lhsT=codes[:, col : col + 128].bitcast(FP8X4),
                lhsT_scale=scales[:, col : col + 128],
                rhs=w_q[(g, hf)][0][:, lo:hi].bitcast(FP8X4),
                rhs_scale=w_q[(g, hf)][1][:, lo:hi],
                start=(g == 0),
                stop=(g == G - 1),
            )
            if g == G - 1:
                finish(hf, m, lo, hi)

        def keep_busy(n):
            for k in range(n):
                nc.tensor.matmul(
                    busy_bank[0][:].rearrange("p (n c) -> p n c", n=4),
                    lhsT=ones[:],
                    rhs=ones[:].unsqueeze(1).to_broadcast([P, 4, P]),
                    start=True,
                    stop=True,
                )

        busy_bank = [None]

        held["busy"] = bank_order[0]
        busy_bank[0] = psum.tile([P, 512], F32, name=bank_order[0], tag=bank_order[0])
        bank_order.remove(held["busy"])
        keep_busy(WARM)

        def spread_s():
            bank = next_bank()
            for k in range(4):
                first_r = 256 * (k // 2) + k % 2
                nc.tensor.matmul(
                    bank[:, k : k + 1], lhsT=s_row[:, first_r : first_r + 255 : 2], rhs=ones[:, 0:1], start=True, stop=True
                )
            nc.scalar.copy(out=s4[:].rearrange("p u e -> p (u e)"), in_=bank[:, 0:4])

        def spread_bias(hf):
            bank = next_bank()
            nc.tensor.matmul(bank[:], lhsT=ones[:, 0:P], rhs=bias_row[:, 512 * hf : 512 * (hf + 1)], start=True, stop=True)
            nc.scalar.copy(out=bias_bc[:, 512 * hf : 512 * (hf + 1)], in_=bank[:])

        def transpose_v_rows(t):
            bank = next_bank()
            for u in range(2):
                nc.tensor.transpose(
                    bank[:, 128 * u : 128 * u + 128],
                    v_sb[0][:].bitcast(F32)[:, 256 * t + 128 * u : 256 * t + 128 * u + 128],
                    ident[:],
                )
            nc.scalar.copy(
                out=vg[:, 512 * t : 512 * (t + 1)].bitcast(F32).rearrange("p (c u) -> p c u", u=2),
                in_=bank[:, 0:256].rearrange("p (u c) -> p c u", u=2),
            )

        ug0 = grouped_tile("usg")
        ug1 = grouped_tile("usg")
        vg = grouped_tile("vg")
        def point(i):
            keep_busy(DUM[i])
            if i == B0:
                spread_bias(0)
            if i == B1:
                spread_bias(1)

        spread_s()
        point(0)
        for half in range(2):
            bank_u = transpose_half(u_sb[half][:])
            scale_bank(bank_u, ug0[:, 1024 * half : 1024 * (half + 1)])
            point(1 + half)
        for t in range(2):
            transpose_v_rows(t)
            point(3 + t)
            quantise(ug0, us_q[0], 256 * t, 256 * (t + 1))
            quantise(vg, v_q[0], 128 * t, 128 * (t + 1))
        bank_v = transpose_half(v_sb[1][:])
        copy_bank_words(bank_v, vg[:, 1024:2048])
        point(5)
        bank_u = transpose_half(u_halves(1)[0])
        scale_bank(bank_u, ug1[:, 0:1024])
        quantise(vg, v_q[0], 256, 512)
        point(6)
        bank_u = transpose_half(u_halves(1)[1])
        scale_bank(bank_u, ug1[:, 1024:2048])
        bank_order.append(held["busy"])
        for t in range(2):
            quantise(ug1, us_q[1], 256 * t, 256 * (t + 1))

        order = [(g, 0) for g in range(G)] + [(g, 1) for g in range(G)]
        slot = {}
        for r, (g, hf) in enumerate(order):
            slot[(g, hf)] = r
        h_ready = {}
        for r in H_ROUND:
            for unit in H_ROUND[r]:
                h_ready[unit] = r

        def is_ready(item, r):
            g, hf, m = item[0], item[1], item[2]
            return r >= slot[(g, hf)] + 2 and r >= h_ready[(g // 2, m // 2)] + 1

        passes = [(g, 0, m) for g in range(G) for m in range(2)]
        first = [(g, 0, m) for g in range(G) for m in range(2, 4)]
        second = [(g, 1, m) for g in range(G) for m in range(2)]
        passes = passes[0:14] + first[0:2] + passes[14:16] + first[2:4]
        for k in range(2, G):
            passes += first[2 * k : 2 * k + 2] + second[2 * k - 4 : 2 * k - 2]
        passes += second[12:14] + [(g, 1, 2) for g in range(G - 1)] + second[14:16] + [(G - 1, 1, 2)]
        passes += [(g, 1, 3, 0, 256) for g in range(G)] + [(g, 1, 3, 256, 384) for g in range(G)] + [(g, 1, 3, 384, 512) for g in range(G)]
        assert len(passes) == 80

        def take(n, r):
            while n > 0 and passes and is_ready(passes[0], r):
                stage2_pass(*passes[0])
                passes.remove(passes[0])
                n = n - 1

        for r, (g, hf) in enumerate(order):
            on_v = COPY_V.get(r, () if hf == 0 else COPY_V_LATE)
            for b in range(4):
                stage1_bank(g, hf, b, b in on_v)
                if hf == 1 and b == 0 and g > 0:
                    quantise_w(g - 1, 1)
                take((TAKE_EARLY if hf == 0 else TAKE_LATE)[b], r)
                if r == V2_ROUND and b == 3:
                    vg = prepare_v2()
            late = []
            units = H_ROUND.get(r, ())
            for k, z in units:
                if z == 1 and k in BLOCKS:
                    late.append((prepare_blocks(h_sb[(k, z)], "hg"), h_q[(k, z)]))
            if r + 2 < G:
                ug = prepare_u(r + 2)
            if hf == 0:
                quantise_w(g, 0)
            for k, z in units:
                if z == 0 or k not in BLOCKS:
                    late.append((prepare_h(k, z), h_q[(k, z)]))
            if r + 2 < G:
                quantise(ug, us_q[r + 2])
            if r == V2_ROUND:
                quantise(vg, v_q[1])
            for grouped, codes in late:
                quantise(grouped, codes)
        quantise_w(G - 1, 1)
        take(len(passes), 99)
